import numpy as np
import ml_dtypes


def mxq(x, axis, fmt="e4m3"):
    dtype, down = {"e4m3": (ml_dtypes.float8_e4m3fn, 7), "e5m2": (ml_dtypes.float8_e5m2, 14)}[fmt]
    v = np.moveaxis(np.asarray(x, np.float32).astype(ml_dtypes.bfloat16).astype(np.float64), axis, -1)
    blocks = v.reshape(v.shape[:-1] + (-1, 32))
    amax = np.abs(blocks).max(-1, keepdims=True)
    byte = np.maximum(np.where(amax > 0, np.frexp(amax)[1] - 1 + 127, 0) - down, 1)
    scale = np.exp2(byte - 127.0)
    codes = (blocks / scale).astype(np.float32).astype(dtype).astype(np.float64)
    return np.moveaxis((codes * scale).reshape(v.shape), -1, axis)


WIDE = False


def mx_kscale(k):
    if not WIDE:
        return np.ones(k)
    levels = np.array([20, -20, 10, -10, 0])
    a = np.random.permutation(np.resize(levels, k // 512 * 4)).reshape(k // 512, 4)
    idx = np.arange(k)
    return np.exp2(a[idx // 512, idx % 128 // 32])


BF16 = ml_dtypes.bfloat16


def bf(x):
    return np.asarray(x, np.float32).astype(BF16)


def f64(x):
    return np.asarray(x).astype(np.float64)


B, NP, H, W, EMB = 4, 128, 16, 32, 512
L = NP + H * W
C2 = EMB + EMB
NT = B * L
BN_EPS = 1e-5


def conv(T1, T2, Wf):
    joint = np.concatenate([f64(T1), f64(T2)], axis=2)
    return joint @ f64(Wf).T


def setup_inputs():
    u = mx_kscale(EMB)
    T1 = bf(np.random.standard_normal((B, L, EMB)))
    T2 = bf(np.random.standard_normal((B, L, EMB)))
    Wf0 = bf(np.random.standard_normal((EMB, C2)) / np.sqrt(C2))
    bn_g = bf(1.0 + 0.1 * np.random.standard_normal(EMB))
    bn_b = bf(0.3 * np.random.standard_normal(EMB))
    g = bf(np.random.standard_normal((B, L, EMB)) * np.exp2(np.random.randint(-12, 1, (B, L, 1))) * 8.0 * u)
    z = conv(T1, T2, Wf0)
    mu = z.mean(axis=(0, 1))
    rstd = 1.0 / np.sqrt(z.var(axis=(0, 1)) + BN_EPS)
    return {'T1': T1, 'T2': T2, 'Wf': bf(f64(Wf0) / u[:, None]), 'bn_g': bn_g, 'bn_b': bn_b,
            'z': np.asarray(z, np.float32), 'mu': np.asarray(mu, np.float32),
            'rstd': np.asarray(rstd, np.float32), 'grad_out': g}


def reference(T1, T2, Wf, bn_g, bn_b, z, mu, rstd, grad_out):
    gam, bet, rs = f64(bn_g), f64(bn_b), f64(rstd)
    xh = ((f64(z) - f64(mu)) * rs).reshape(NT, EMB)
    g = f64(grad_out).reshape(NT, EMB)
    dh = g * (xh * gam + bet > 0.0) * gam
    m1 = dh.mean(axis=0)
    m2 = (dh * xh).mean(axis=0)
    dz = rs * (dh - m1 - xh * m2)
    gx = mxq(dz, 1, 'e5m2') @ mxq(f64(Wf)[:, :EMB], 0, 'e4m3')
    return gx.reshape(B, L, EMB)

@@ -1,0 +1,204 @@
+from contextlib import ExitStack
+
+import concourse.mybir as mybir
+from concourse.masks import make_identity
+
+F32 = mybir.dt.float32
+BF16 = mybir.dt.bfloat16
+U32 = mybir.dt.uint32
+U8 = mybir.dt.uint8
+E5M2_X4 = mybir.dt.float8_e5m2_x4
+E4M3_X4 = mybir.dt.float8_e4m3fn_x4
+ALU = mybir.AluOpType
+ACT = mybir.ActivationFunctionType
+AXIS = mybir.AxisListType
+
+P = 128
+PACK = 4
+EMB = 512
+ROWS = 4 * 640
+TILES = 4
+CHUNK = TILES * P
+CHUNKS = ROWS // CHUNK
+RUN = 4
+
+FLOPS = 2 * ROWS * EMB * EMB
+BYTES = ROWS * EMB * (4 + 2 + 4) + EMB * EMB * 2 + EMB * (4 + 4 + 2 + 2)
+
+
+def regroup(nc, grouped, planes):
+    nc.vector.tensor_copy(
+        out=grouped.rearrange("p (c i) t -> p c t i", i=RUN),
+        in_=planes.rearrange("p t (c i) -> p c t i", i=RUN),
+    )
+
+
+def tile_iag_pb_v_kernel(tc, T1, T2, Wf, bn_g, bn_b, z, mu, rstd, grad_out, out):
+    nc = tc.nc
+
+    z_chunks = z.flatten_outer_dims().rearrange("(c p j) o -> c p j o", p=P, j=TILES)
+    g_chunks = grad_out.flatten_outer_dims().rearrange("(c p j) o -> c p j o", p=P, j=TILES)
+    out_tiles = out.flatten_outer_dims().rearrange("(c p j) o -> c j p o", p=P, j=TILES)
+
+    with ExitStack() as ctx:
+        const = ctx.enter_context(tc.tile_pool(name="const", bufs=1))
+        resident = ctx.enter_context(tc.tile_pool(name="resident", bufs=CHUNKS))
+        stream = ctx.enter_context(tc.tile_pool(name="stream", bufs=4))
+        stage = ctx.enter_context(tc.tile_pool(name="stage", bufs=2))
+        psum = ctx.enter_context(tc.psum_pool(name="psum", bufs=4))
+
+        rows_f32 = const.tile([P, P], F32)
+        rows_bf16 = const.tile([P, P], BF16)
+        nc.vector.memset(rows_f32[:], 0.0)
+        nc.vector.memset(rows_bf16[:], 0.0)
+        nc.scalar.dma_start(out=rows_f32[0:PACK, :], in_=mu.rearrange("(t p) -> t p", p=P))
+        nc.scalar.dma_start(out=rows_f32[PACK : 2 * PACK, :], in_=rstd.rearrange("(t p) -> t p", p=P))
+        nc.scalar.dma_start(out=rows_bf16[0:PACK, :], in_=bn_g.rearrange("(t p) -> t p", p=P))
+        nc.scalar.dma_start(out=rows_bf16[PACK : 2 * PACK, :], in_=bn_b.rearrange("(t p) -> t p", p=P))
+
+        z_in = []
+        g_in = []
+        for c in range(CHUNKS):
+            z_in.append(resident.tile([P, TILES, EMB], F32, name="z_in"))
+            g_in.append(resident.tile([P, TILES, EMB], BF16, name="g_in"))
+            nc.sync.dma_start(out=z_in[c][:], in_=z_chunks[c])
+            nc.sync.dma_start(out=g_in[c][:], in_=g_chunks[c])
+        w_planes = const.tile([P, PACK, EMB], BF16)
+        nc.sync.dma_start(out=w_planes[:], in_=Wf.rearrange("(t p) c -> p t c", p=P)[:, :, 0:EMB])
+
+        ident_f32 = const.tile([P, P], F32)
+        ident_bf16 = const.tile([P, P], BF16)
+        make_identity(nc, ident_f32[:])
+        make_identity(nc, ident_bf16[:])
+
+        cols_f32 = psum.tile([P, P], F32, tag="f32_bank")
+        cols_bf16 = psum.tile([P, P], BF16, tag="bf16_bank")
+        nc.tensor.transpose(out=cols_f32[:], in_=rows_f32[:], identity=ident_f32[:])
+        nc.tensor.transpose(out=cols_bf16[:], in_=rows_bf16[:], identity=ident_bf16[:])
+        saved = const.tile([P, 2 * PACK], F32)
+        affine = const.tile([P, 2 * PACK], F32)
+        nc.vector.tensor_copy(out=saved[:], in_=cols_f32[:, 0 : 2 * PACK])
+        nc.vector.tensor_copy(out=affine[:], in_=cols_bf16[:, 0 : 2 * PACK])
+        mean = saved[:, 0:PACK]
+        inv_std = saved[:, PACK : 2 * PACK]
+        gamma = affine[:, 0:PACK]
+        beta = affine[:, PACK : 2 * PACK]
+
+        xh_bias = const.tile([P, PACK], F32)
+        gain = const.tile([P, PACK], F32)
+        y_bias = const.tile([P, PACK], F32)
+        nc.vector.scalar_tensor_tensor(
+            out=xh_bias[:], in0=mean, scalar=-1.0, in1=inv_std, op0=ALU.mult, op1=ALU.mult
+        )
+        nc.vector.tensor_mul(out=gain[:], in0=inv_std, in1=gamma)
+        nc.vector.tensor_mul(out=y_bias[:], in0=xh_bias[:], in1=gamma)
+        nc.vector.tensor_add(out=y_bias[:], in0=y_bias[:], in1=beta)
+
+        xh = [resident.tile([P, PACK, CHUNK], F32, name="xh") for c in range(CHUNKS)]
+        gm = [resident.tile([P, PACK, CHUNK], BF16, name="gm") for c in range(CHUNKS)]
+        sum_gm = const.tile([P, PACK, CHUNKS], F32)
+        sum_gx = const.tile([P, PACK, CHUNKS], F32)
+
+        def mask_gradient(c, t):
+            channels = slice(t * P, (t + 1) * P)
+            z_t = psum.tile([P, CHUNK], F32, tag="f32_bank")
+            g_t = psum.tile([P, CHUNK], BF16, tag="bf16_bank")
+            for j in range(TILES):
+                nc.tensor.transpose(
+                    out=z_t[:, j * P : (j + 1) * P], in_=z_in[c][:, j, channels], identity=ident_f32[:]
+                )
+            for j in range(TILES):
+                nc.tensor.transpose(
+                    out=g_t[:, j * P : (j + 1) * P], in_=g_in[c][:, j, channels], identity=ident_bf16[:]
+                )
+            nc.scalar.activation(
+                out=xh[c][:, t, :], in_=z_t[:], func=ACT.Identity,
+                scale=inv_std[:, t : t + 1], bias=xh_bias[:, t : t + 1],
+            )
+            y = stream.tile([P, CHUNK], BF16)
+            nc.scalar.activation(
+                out=y[:], in_=z_t[:], func=ACT.Identity,
+                scale=gain[:, t : t + 1], bias=y_bias[:, t : t + 1],
+            )
+            nc.vector.scalar_tensor_tensor(
+                out=gm[c][:, t, :], in0=y[:], scalar=0.0, in1=g_t[:], op0=ALU.is_gt, op1=ALU.mult,
+                accum_out=sum_gm[:, t, c : c + 1],
+            )
+
+        def correlate(c, t):
+            product = stream.tile([P, CHUNK], F32)
+            nc.vector.scalar_tensor_tensor(
+                out=product[:], in0=gm[c][:, t, :], scalar=gain[:, t : t + 1], in1=xh[c][:, t, :],
+                op0=ALU.mult, op1=ALU.mult, accum_out=sum_gx[:, t, c : c + 1],
+            )
+
+        steps = [(c, t) for c in range(CHUNKS) for t in range(PACK)]
+        for i in range(len(steps)):
+            mask_gradient(*steps[i])
+            if i > 0:
+                correlate(*steps[i - 1])
+        correlate(*steps[-1])
+
+        total_gm = const.tile([P, PACK], F32)
+        total_gx = const.tile([P, PACK], F32)
+        shift = const.tile([P, PACK], F32)
+        slope = const.tile([P, PACK], F32)
+        nc.vector.reduce_sum(out=total_gm[:], in_=sum_gm[:], axis=AXIS.X)
+        nc.vector.reduce_sum(out=total_gx[:], in_=sum_gx[:], axis=AXIS.X)
+        nc.vector.scalar_tensor_tensor(
+            out=shift[:], in0=total_gm[:], scalar=-1.0 / ROWS, in1=gain[:], op0=ALU.mult, op1=ALU.mult
+        )
+        nc.vector.tensor_scalar_mul(out=slope[:], in0=total_gx[:], scalar1=-1.0 / ROWS)
+
+        w_grouped = const.tile([P, EMB, PACK], BF16, align_bytes=64)
+        w_codes = const.tile([P, EMB], U32, align_bytes=64)
+        w_scales = const.tile([P, EMB], U8, align_bytes=64)
+        regroup(nc, w_grouped[:], w_planes[:])
+        nc.vector.quantize_mx(
+            out=w_codes[:].bitcast(E4M3_X4), scales=w_scales[:],
+            in_=w_grouped[:].rearrange("p c t -> p (c t)"),
+        )
+
+        dz_grouped = []
+        def gradient(c):
+            means_term = stage.tile([P, PACK, CHUNK], F32)
+            dz_planes = stage.tile([P, PACK, CHUNK], BF16)
+            for t in range(PACK):
+                nc.scalar.activation(
+                    out=means_term[:, t, :], in_=xh[c][:, t, :], func=ACT.Identity,
+                    scale=slope[:, t : t + 1], bias=shift[:, t : t + 1],
+                )
+            for t in range(PACK):
+                nc.vector.scalar_tensor_tensor(
+                    out=dz_planes[:, t, :], in0=gm[c][:, t, :], scalar=gain[:, t : t + 1],
+                    in1=means_term[:, t, :], op0=ALU.mult, op1=ALU.add,
+                )
+            return dz_planes
+
+        def multiply(c):
+            dz_codes = stage.tile([P, CHUNK], U32, align_bytes=64)
+            dz_scales = stage.tile([P, CHUNK], U8, align_bytes=64)
+            nc.vector.quantize_mx(
+                out=dz_codes[:].bitcast(E5M2_X4), scales=dz_scales[:],
+                in_=dz_grouped[c][:].rearrange("p w t -> p (w t)"),
+            )
+            for j in range(TILES):
+                rows = slice(j * P, (j + 1) * P)
+                acc = psum.tile([P, EMB], F32, tag="f32_bank")
+                nc.tensor.matmul_mx(
+                    out=acc[:],
+                    lhsT=dz_codes[:, rows].bitcast(E5M2_X4), lhsT_scale=dz_scales[:, rows],
+                    rhs=w_codes[:].bitcast(E4M3_X4), rhs_scale=w_scales[:],
+                    start=True, stop=True,
+                )
+                result = stream.tile([P, EMB], F32)
+                nc.scalar.copy(out=result[:], in_=acc[:])
+                nc.sync.dma_start(out=out_tiles[c, j], in_=result[:])
+
+        for c in range(CHUNKS):
+            dz_planes = gradient(c)
+            if c > 0:
+                multiply(c - 1)
+            dz_grouped.append(stage.tile([P, CHUNK, PACK], BF16, name="dz_grouped", align_bytes=64))
+            regroup(nc, dz_grouped[c][:], dz_planes[:])
+        multiply(CHUNKS - 1)

@@ -21,13 +21,14 @@ TILES = 4
 CHUNK = TILES * P
 CHUNKS = ROWS // CHUNK
 RUN = 4
+AHEAD = 2
 
 FLOPS = 2 * ROWS * EMB * EMB
 BYTES = ROWS * EMB * (4 + 2 + 4) + EMB * EMB * 2 + EMB * (4 + 4 + 2 + 2)
 
 
-def regroup(nc, grouped, planes):
-    nc.vector.tensor_copy(
+def regroup(copy, grouped, planes):
+    copy(
         out=grouped.rearrange("p (c i) t -> p c t i", i=RUN),
         in_=planes.rearrange("p t (c i) -> p c t i", i=RUN),
     )
@@ -49,12 +50,12 @@ def tile_iag_pb_v_kernel(tc, T1, T2, Wf, bn_g, bn_b, z, mu, rstd, grad_out, out)
 
         rows_f32 = const.tile([P, P], F32)
         rows_bf16 = const.tile([P, P], BF16)
-        nc.vector.memset(rows_f32[:], 0.0)
-        nc.vector.memset(rows_bf16[:], 0.0)
-        nc.scalar.dma_start(out=rows_f32[0:PACK, :], in_=mu.rearrange("(t p) -> t p", p=P))
-        nc.scalar.dma_start(out=rows_f32[PACK : 2 * PACK, :], in_=rstd.rearrange("(t p) -> t p", p=P))
-        nc.scalar.dma_start(out=rows_bf16[0:PACK, :], in_=bn_g.rearrange("(t p) -> t p", p=P))
-        nc.scalar.dma_start(out=rows_bf16[PACK : 2 * PACK, :], in_=bn_b.rearrange("(t p) -> t p", p=P))
+        nc.gpsimd.memset(rows_f32[:], 0.0)
+        nc.gpsimd.memset(rows_bf16[:], 0.0)
+        nc.sync.dma_start(out=rows_f32[0:PACK, :], in_=mu.rearrange("(t p) -> t p", p=P))
+        nc.sync.dma_start(out=rows_f32[PACK : 2 * PACK, :], in_=rstd.rearrange("(t p) -> t p", p=P))
+        nc.sync.dma_start(out=rows_bf16[0:PACK, :], in_=bn_g.rearrange("(t p) -> t p", p=P))
+        nc.sync.dma_start(out=rows_bf16[PACK : 2 * PACK, :], in_=bn_b.rearrange("(t p) -> t p", p=P))
 
         z_in = []
         g_in = []
@@ -139,6 +140,11 @@ def tile_iag_pb_v_kernel(tc, T1, T2, Wf, bn_g, bn_b, z, mu, rstd, grad_out, out)
                 correlate(*steps[i - 1])
         correlate(*steps[-1])
 
+        w_grouped = const.tile([P, EMB, PACK], BF16, align_bytes=64)
+        w_codes = const.tile([P, EMB], U32, align_bytes=64)
+        w_scales = const.tile([P, EMB], U8, align_bytes=64)
+        regroup(nc.scalar.copy, w_grouped[:], w_planes[:])
+
         total_gm = const.tile([P, PACK], F32)
         total_gx = const.tile([P, PACK], F32)
         shift = const.tile([P, PACK], F32)
@@ -150,30 +156,23 @@ def tile_iag_pb_v_kernel(tc, T1, T2, Wf, bn_g, bn_b, z, mu, rstd, grad_out, out)
         )
         nc.vector.tensor_scalar_mul(out=slope[:], in0=total_gx[:], scalar1=-1.0 / ROWS)
 
-        w_grouped = const.tile([P, EMB, PACK], BF16, align_bytes=64)
-        w_codes = const.tile([P, EMB], U32, align_bytes=64)
-        w_scales = const.tile([P, EMB], U8, align_bytes=64)
-        regroup(nc, w_grouped[:], w_planes[:])
-        nc.vector.quantize_mx(
-            out=w_codes[:].bitcast(E4M3_X4), scales=w_scales[:],
-            in_=w_grouped[:].rearrange("p c t -> p (c t)"),
-        )
-
-        dz_grouped = []
-        def gradient(c):
-            means_term = stage.tile([P, PACK, CHUNK], F32)
-            dz_planes = stage.tile([P, PACK, CHUNK], BF16)
+        def means_term(c):
             for t in range(PACK):
                 nc.scalar.activation(
-                    out=means_term[:, t, :], in_=xh[c][:, t, :], func=ACT.Identity,
+                    out=xh[c][:, t, :], in_=xh[c][:, t, :], func=ACT.Identity,
                     scale=slope[:, t : t + 1], bias=shift[:, t : t + 1],
                 )
+
+        def gradient(c):
+            dz_planes = stage.tile([P, PACK, CHUNK], BF16)
             for t in range(PACK):
                 nc.vector.scalar_tensor_tensor(
                     out=dz_planes[:, t, :], in0=gm[c][:, t, :], scalar=gain[:, t : t + 1],
-                    in1=means_term[:, t, :], op0=ALU.mult, op1=ALU.add,
+                    in1=xh[c][:, t, :], op0=ALU.mult, op1=ALU.add,
                 )
             return dz_planes
+
+        dz_grouped = []
 
         def multiply(c):
             dz_codes = stage.tile([P, CHUNK], U32, align_bytes=64)
@@ -182,6 +181,7 @@ def tile_iag_pb_v_kernel(tc, T1, T2, Wf, bn_g, bn_b, z, mu, rstd, grad_out, out)
                 out=dz_codes[:].bitcast(E5M2_X4), scales=dz_scales[:],
                 in_=dz_grouped[c][:].rearrange("p w t -> p (w t)"),
             )
+            vector_helps = c == CHUNKS - 1
             for j in range(TILES):
                 rows = slice(j * P, (j + 1) * P)
                 acc = psum.tile([P, EMB], F32, tag="f32_bank")
@@ -192,13 +192,25 @@ def tile_iag_pb_v_kernel(tc, T1, T2, Wf, bn_g, bn_b, z, mu, rstd, grad_out, out)
                     start=True, stop=True,
                 )
                 result = stream.tile([P, EMB], F32)
-                nc.scalar.copy(out=result[:], in_=acc[:])
+                if vector_helps and j % 2 == 1:
+                    nc.vector.tensor_copy(out=result[:], in_=acc[:])
+                else:
+                    nc.scalar.copy(out=result[:], in_=acc[:])
                 nc.sync.dma_start(out=out_tiles[c, j], in_=result[:])
 
+        for c in range(AHEAD):
+            means_term(c)
         for c in range(CHUNKS):
+            if c + AHEAD < CHUNKS:
+                means_term(c + AHEAD)
             dz_planes = gradient(c)
-            if c > 0:
+            if c == 0:
+                nc.vector.quantize_mx(
+                    out=w_codes[:].bitcast(E4M3_X4), scales=w_scales[:],
+                    in_=w_grouped[:].rearrange("p c t -> p (c t)"),
+                )
+            else:
                 multiply(c - 1)
             dz_grouped.append(stage.tile([P, CHUNK, PACK], BF16, name="dz_grouped", align_bytes=64))
-            regroup(nc, dz_grouped[c][:], dz_planes[:])
+            regroup(nc.vector.tensor_copy, dz_grouped[c][:], dz_planes[:])
         multiply(CHUNKS - 1)

@@ -21,17 +21,22 @@ TILES = 4
 CHUNK = TILES * P
 CHUNKS = ROWS // CHUNK
 RUN = 4
+VECTOR_PLANES = 1
+VECTOR_BANKS = 1
+SCALAR_PLANES = PACK - VECTOR_PLANES
+SCALAR_BANKS = TILES - VECTOR_BANKS
 AHEAD = 2
 
 FLOPS = 2 * ROWS * EMB * EMB
 BYTES = ROWS * EMB * (4 + 2 + 4) + EMB * EMB * 2 + EMB * (4 + 4 + 2 + 2)
 
 
-def regroup(copy, grouped, planes):
-    copy(
-        out=grouped.rearrange("p (c i) t -> p c t i", i=RUN),
-        in_=planes.rearrange("p t (c i) -> p c t i", i=RUN),
-    )
+def by_word(planes):
+    return planes.rearrange("p t (c i) -> p c t i", i=RUN)
+
+
+def as_words(grouped):
+    return grouped.rearrange("p (c i) t -> p c t i", i=RUN)
 
 
 def tile_iag_pb_v_kernel(tc, T1, T2, Wf, bn_g, bn_b, z, mu, rstd, grad_out, out):
@@ -42,11 +47,13 @@ def tile_iag_pb_v_kernel(tc, T1, T2, Wf, bn_g, bn_b, z, mu, rstd, grad_out, out)
     out_tiles = out.flatten_outer_dims().rearrange("(c p j) o -> c j p o", p=P, j=TILES)
 
     with ExitStack() as ctx:
+        ctx.enter_context(tc.manual_schedule())
         const = ctx.enter_context(tc.tile_pool(name="const", bufs=1))
         resident = ctx.enter_context(tc.tile_pool(name="resident", bufs=CHUNKS))
         stream = ctx.enter_context(tc.tile_pool(name="stream", bufs=4))
         stage = ctx.enter_context(tc.tile_pool(name="stage", bufs=2))
-        psum = ctx.enter_context(tc.psum_pool(name="psum", bufs=4))
+        outgoing = ctx.enter_context(tc.tile_pool(name="outgoing", bufs=2 * TILES))
+        psum = ctx.enter_context(tc.psum_pool(name="psum", bufs=5))
 
         rows_f32 = const.tile([P, P], F32)
         rows_bf16 = const.tile([P, P], BF16)
@@ -73,37 +80,50 @@ def tile_iag_pb_v_kernel(tc, T1, T2, Wf, bn_g, bn_b, z, mu, rstd, grad_out, out)
         make_identity(nc, ident_bf16[:])
 
         cols_f32 = psum.tile([P, P], F32, tag="f32_bank")
-        cols_bf16 = psum.tile([P, P], BF16, tag="bf16_bank")
+        cols_bf16 = psum.tile([P, P], BF16, tag="bf16_bank", bufs=3)
         nc.tensor.transpose(out=cols_f32[:], in_=rows_f32[:], identity=ident_f32[:])
         nc.tensor.transpose(out=cols_bf16[:], in_=rows_bf16[:], identity=ident_bf16[:])
         saved = const.tile([P, 2 * PACK], F32)
         affine = const.tile([P, 2 * PACK], F32)
-        nc.vector.tensor_copy(out=saved[:], in_=cols_f32[:, 0 : 2 * PACK])
         nc.vector.tensor_copy(out=affine[:], in_=cols_bf16[:, 0 : 2 * PACK])
+        nc.vector.tensor_copy(out=saved[:], in_=cols_f32[:, 0 : 2 * PACK])
         mean = saved[:, 0:PACK]
         inv_std = saved[:, PACK : 2 * PACK]
         gamma = affine[:, 0:PACK]
         beta = affine[:, PACK : 2 * PACK]
 
-        xh_bias = const.tile([P, PACK], F32)
+        half_sign = const.tile([P, PACK], F32)
+        xs_scale = const.tile([P, PACK], F32)
+        xs_bias = const.tile([P, PACK], F32)
         gain = const.tile([P, PACK], F32)
-        y_bias = const.tile([P, PACK], F32)
+        threshold = const.tile([P, PACK], F32)
+        nc.vector.tensor_scalar(
+            out=half_sign[:], in0=gamma, scalar1=0.0, scalar2=0.5, op0=ALU.is_ge, op1=ALU.subtract
+        )
         nc.vector.scalar_tensor_tensor(
-            out=xh_bias[:], in0=mean, scalar=-1.0, in1=inv_std, op0=ALU.mult, op1=ALU.mult
+            out=xs_scale[:], in0=half_sign[:], scalar=2.0, in1=inv_std, op0=ALU.mult, op1=ALU.mult
         )
         nc.vector.tensor_mul(out=gain[:], in0=inv_std, in1=gamma)
-        nc.vector.tensor_mul(out=y_bias[:], in0=xh_bias[:], in1=gamma)
-        nc.vector.tensor_add(out=y_bias[:], in0=y_bias[:], in1=beta)
+        nc.vector.scalar_tensor_tensor(
+            out=xs_bias[:], in0=mean, scalar=-1.0, in1=xs_scale[:], op0=ALU.mult, op1=ALU.mult
+        )
+        nc.vector.scalar_tensor_tensor(
+            out=threshold[:], in0=half_sign[:], scalar=2.0, in1=gamma, op0=ALU.mult, op1=ALU.mult
+        )
+        nc.vector.reciprocal(out=threshold[:], in_=threshold[:])
+        nc.vector.scalar_tensor_tensor(
+            out=threshold[:], in0=beta, scalar=-1.0, in1=threshold[:], op0=ALU.mult, op1=ALU.mult
+        )
 
-        xh = [resident.tile([P, PACK, CHUNK], F32, name="xh") for c in range(CHUNKS)]
-        gm = [resident.tile([P, PACK, CHUNK], BF16, name="gm") for c in range(CHUNKS)]
-        sum_gm = const.tile([P, PACK, CHUNKS], F32)
+        xs = [resident.tile([P, PACK, CHUNK], F32, name="xs") for c in range(CHUNKS)]
+        gma = [resident.tile([P, PACK, CHUNK], F32, name="gma") for c in range(CHUNKS)]
+        sum_g = const.tile([P, PACK, CHUNKS], F32)
         sum_gx = const.tile([P, PACK, CHUNKS], F32)
 
         def mask_gradient(c, t):
             channels = slice(t * P, (t + 1) * P)
             z_t = psum.tile([P, CHUNK], F32, tag="f32_bank")
-            g_t = psum.tile([P, CHUNK], BF16, tag="bf16_bank")
+            g_t = psum.tile([P, CHUNK], BF16, tag="bf16_bank", bufs=3)
             for j in range(TILES):
                 nc.tensor.transpose(
                     out=z_t[:, j * P : (j + 1) * P], in_=z_in[c][:, j, channels], identity=ident_f32[:]
@@ -113,75 +133,101 @@ def tile_iag_pb_v_kernel(tc, T1, T2, Wf, bn_g, bn_b, z, mu, rstd, grad_out, out)
                     out=g_t[:, j * P : (j + 1) * P], in_=g_in[c][:, j, channels], identity=ident_bf16[:]
                 )
             nc.scalar.activation(
-                out=xh[c][:, t, :], in_=z_t[:], func=ACT.Identity,
-                scale=inv_std[:, t : t + 1], bias=xh_bias[:, t : t + 1],
+                out=xs[c][:, t, :], in_=z_t[:], func=ACT.Identity,
+                scale=xs_scale[:, t : t + 1], bias=xs_bias[:, t : t + 1],
             )
-            y = stream.tile([P, CHUNK], BF16)
-            nc.scalar.activation(
-                out=y[:], in_=z_t[:], func=ACT.Identity,
-                scale=gain[:, t : t + 1], bias=y_bias[:, t : t + 1],
-            )
+            g_scaled = stream.tile([P, CHUNK], F32)
+            nc.scalar.activation(out=g_scaled[:], in_=g_t[:], func=ACT.Identity, scale=gain[:, t : t + 1])
             nc.vector.scalar_tensor_tensor(
-                out=gm[c][:, t, :], in0=y[:], scalar=0.0, in1=g_t[:], op0=ALU.is_gt, op1=ALU.mult,
-                accum_out=sum_gm[:, t, c : c + 1],
+                out=gma[c][:, t, :], in0=xs[c][:, t, :], scalar=threshold[:, t : t + 1], in1=g_scaled[:],
+                op0=ALU.is_gt, op1=ALU.mult, accum_out=sum_g[:, t, c : c + 1],
             )
 
         def correlate(c, t):
             product = stream.tile([P, CHUNK], F32)
             nc.vector.scalar_tensor_tensor(
-                out=product[:], in0=gm[c][:, t, :], scalar=gain[:, t : t + 1], in1=xh[c][:, t, :],
+                out=product[:], in0=gma[c][:, t, :], scalar=1.0, in1=xs[c][:, t, :],
                 op0=ALU.mult, op1=ALU.mult, accum_out=sum_gx[:, t, c : c + 1],
+            )
+
+        w_grouped = const.tile([P, EMB, PACK], BF16, align_bytes=64)
+        w_codes = const.tile([P, EMB], U32, align_bytes=64)
+        w_scales = const.tile([P, EMB], U8, align_bytes=64)
+
+        def quantise_weights():
+            nc.scalar.copy(out=as_words(w_grouped[:]), in_=by_word(w_planes[:]))
+            nc.vector.quantize_mx(
+                out=w_codes[:].bitcast(E4M3_X4), scales=w_scales[:],
+                in_=w_grouped[:].rearrange("p c t -> p (c t)"),
             )
 
         steps = [(c, t) for c in range(CHUNKS) for t in range(PACK)]
         for i in range(len(steps)):
+            if steps[i] == (CHUNKS - 1, 0):
+                quantise_weights()
             mask_gradient(*steps[i])
             if i > 0:
                 correlate(*steps[i - 1])
         correlate(*steps[-1])
 
-        w_grouped = const.tile([P, EMB, PACK], BF16, align_bytes=64)
-        w_codes = const.tile([P, EMB], U32, align_bytes=64)
-        w_scales = const.tile([P, EMB], U8, align_bytes=64)
-        regroup(nc.scalar.copy, w_grouped[:], w_planes[:])
+        shift = [const.tile([P, 1], F32, name="shift%d" % t) for t in range(PACK)]
+        slope = [const.tile([P, 1], F32, name="slope%d" % t) for t in range(PACK)]
 
-        total_gm = const.tile([P, PACK], F32)
-        total_gx = const.tile([P, PACK], F32)
-        shift = const.tile([P, PACK], F32)
-        slope = const.tile([P, PACK], F32)
-        nc.vector.reduce_sum(out=total_gm[:], in_=sum_gm[:], axis=AXIS.X)
-        nc.vector.reduce_sum(out=total_gx[:], in_=sum_gx[:], axis=AXIS.X)
-        nc.vector.scalar_tensor_tensor(
-            out=shift[:], in0=total_gm[:], scalar=-1.0 / ROWS, in1=gain[:], op0=ALU.mult, op1=ALU.mult
-        )
-        nc.vector.tensor_scalar_mul(out=slope[:], in0=total_gx[:], scalar1=-1.0 / ROWS)
+        def finish_plane(t):
+            for sums, scalar in ((sum_g, shift[t]), (sum_gx, slope[t])):
+                if t < SCALAR_PLANES:
+                    scaled = stream.tile([P, CHUNKS], F32)
+                    nc.scalar.activation(
+                        out=scaled[:], in_=sums[:, t, :], func=ACT.Identity,
+                        scale=-1.0 / ROWS, accum_out=scalar[:],
+                    )
+                else:
+                    total = stream.tile([P, 1], F32)
+                    nc.vector.reduce_sum(out=total[:], in_=sums[:, t, :], axis=AXIS.X)
+                    nc.vector.tensor_scalar_mul(out=scalar[:], in0=total[:], scalar1=-1.0 / ROWS)
 
-        def means_term(c):
-            for t in range(PACK):
+        def means_term(c, t):
+            if t < SCALAR_PLANES:
                 nc.scalar.activation(
-                    out=xh[c][:, t, :], in_=xh[c][:, t, :], func=ACT.Identity,
-                    scale=slope[:, t : t + 1], bias=shift[:, t : t + 1],
+                    out=xs[c][:, t, :], in_=xs[c][:, t, :], func=ACT.Identity,
+                    scale=slope[t][:], bias=shift[t][:],
+                )
+            else:
+                nc.vector.tensor_scalar(
+                    out=xs[c][:, t, :], in0=xs[c][:, t, :], scalar1=slope[t][:],
+                    scalar2=shift[t][:], op0=ALU.mult, op1=ALU.add,
                 )
 
-        def gradient(c):
-            dz_planes = stage.tile([P, PACK, CHUNK], BF16)
+        def empty(c, j, acc, copy):
+            result = outgoing.tile([P, EMB], F32)
+            copy(out=result[:], in_=acc[:])
+            nc.sync.dma_start(out=out_tiles[c, j], in_=result[:])
+
+        for t in range(PACK):
+            finish_plane(t)
+            means_term(0, t)
+        for c in range(1, AHEAD):
             for t in range(PACK):
-                nc.vector.scalar_tensor_tensor(
-                    out=dz_planes[:, t, :], in0=gm[c][:, t, :], scalar=gain[:, t : t + 1],
-                    in1=xh[c][:, t, :], op0=ALU.mult, op1=ALU.add,
-                )
-            return dz_planes
+                means_term(c, t)
 
-        dz_grouped = []
-
-        def multiply(c):
+        vector_banks = []
+        for c in range(CHUNKS):
+            dz_grouped = stage.tile([P, CHUNK, PACK], BF16, align_bytes=64)
+            nc.vector.tensor_tensor(
+                out=as_words(dz_grouped[:]), in0=by_word(gma[c][:]), in1=by_word(xs[c][:]), op=ALU.add
+            )
+            if c + AHEAD < CHUNKS:
+                for t in range(PACK):
+                    means_term(c + AHEAD, t)
             dz_codes = stage.tile([P, CHUNK], U32, align_bytes=64)
             dz_scales = stage.tile([P, CHUNK], U8, align_bytes=64)
             nc.vector.quantize_mx(
                 out=dz_codes[:].bitcast(E5M2_X4), scales=dz_scales[:],
-                in_=dz_grouped[c][:].rearrange("p w t -> p (w t)"),
+                in_=dz_grouped[:].rearrange("p w t -> p (w t)"),
             )
-            vector_helps = c == CHUNKS - 1
+            for j, acc in vector_banks:
+                empty(c - 1, j, acc, nc.vector.tensor_copy)
+            vector_banks = []
             for j in range(TILES):
                 rows = slice(j * P, (j + 1) * P)
                 acc = psum.tile([P, EMB], F32, tag="f32_bank")
@@ -191,26 +237,9 @@ def tile_iag_pb_v_kernel(tc, T1, T2, Wf, bn_g, bn_b, z, mu, rstd, grad_out, out)
                     rhs=w_codes[:].bitcast(E4M3_X4), rhs_scale=w_scales[:],
                     start=True, stop=True,
                 )
-                result = stream.tile([P, EMB], F32)
-                if vector_helps and j % 2 == 1:
-                    nc.vector.tensor_copy(out=result[:], in_=acc[:])
+                if j < SCALAR_BANKS:
+                    empty(c, j, acc, nc.scalar.copy)
                 else:
-                    nc.scalar.copy(out=result[:], in_=acc[:])
-                nc.sync.dma_start(out=out_tiles[c, j], in_=result[:])
-
-        for c in range(AHEAD):
-            means_term(c)
-        for c in range(CHUNKS):
-            if c + AHEAD < CHUNKS:
-                means_term(c + AHEAD)
-            dz_planes = gradient(c)
-            if c == 0:
-                nc.vector.quantize_mx(
-                    out=w_codes[:].bitcast(E4M3_X4), scales=w_scales[:],
-                    in_=w_grouped[:].rearrange("p c t -> p (c t)"),
-                )
-            else:
-                multiply(c - 1)
-            dz_grouped.append(stage.tile([P, CHUNK, PACK], BF16, name="dz_grouped", align_bytes=64))
-            regroup(nc.vector.tensor_copy, dz_grouped[c][:], dz_planes[:])
-        multiply(CHUNKS - 1)
+                    vector_banks.append((j, acc))
+        for j, acc in vector_banks:
+            empty(CHUNKS - 1, j, acc, nc.vector.tensor_copy)

@@ -69,8 +69,11 @@ def tile_iag_pb_v_kernel(tc, T1, T2, Wf, bn_g, bn_b, z, mu, rstd, grad_out, out)
         for c in range(CHUNKS):
             z_in.append(resident.tile([P, TILES, EMB], F32, name="z_in"))
             g_in.append(resident.tile([P, TILES, EMB], BF16, name="g_in"))
-            nc.sync.dma_start(out=z_in[c][:], in_=z_chunks[c])
-            nc.sync.dma_start(out=g_in[c][:], in_=g_chunks[c])
+            pieces = 2 if c == 0 else 1
+            for k in range(pieces):
+                columns = slice(k * EMB // pieces, (k + 1) * EMB // pieces)
+                nc.sync.dma_start(out=z_in[c][:, :, columns], in_=z_chunks[c][:, :, columns])
+                nc.sync.dma_start(out=g_in[c][:, :, columns], in_=g_chunks[c][:, :, columns])
         w_planes = const.tile([P, PACK, EMB], BF16)
         nc.sync.dma_start(out=w_planes[:], in_=Wf.rearrange("(t p) c -> p t c", p=P)[:, :, 0:EMB])
 
@@ -86,7 +89,7 @@ def tile_iag_pb_v_kernel(tc, T1, T2, Wf, bn_g, bn_b, z, mu, rstd, grad_out, out)
         saved = const.tile([P, 2 * PACK], F32)
         affine = const.tile([P, 2 * PACK], F32)
         nc.vector.tensor_copy(out=affine[:], in_=cols_bf16[:, 0 : 2 * PACK])
-        nc.vector.tensor_copy(out=saved[:], in_=cols_f32[:, 0 : 2 * PACK])
+        nc.scalar.copy(out=saved[:], in_=cols_f32[:, 0 : 2 * PACK])
         mean = saved[:, 0:PACK]
         inv_std = saved[:, PACK : 2 * PACK]
         gamma = affine[:, 0:PACK]
@@ -103,10 +106,10 @@ def tile_iag_pb_v_kernel(tc, T1, T2, Wf, bn_g, bn_b, z, mu, rstd, grad_out, out)
         nc.vector.scalar_tensor_tensor(
             out=xs_scale[:], in0=half_sign[:], scalar=2.0, in1=inv_std, op0=ALU.mult, op1=ALU.mult
         )
-        nc.vector.tensor_mul(out=gain[:], in0=inv_std, in1=gamma)
         nc.vector.scalar_tensor_tensor(
             out=xs_bias[:], in0=mean, scalar=-1.0, in1=xs_scale[:], op0=ALU.mult, op1=ALU.mult
         )
+        nc.vector.tensor_mul(out=gain[:], in0=inv_std, in1=gamma)
         nc.vector.scalar_tensor_tensor(
             out=threshold[:], in0=half_sign[:], scalar=2.0, in1=gamma, op0=ALU.mult, op1=ALU.mult
         )
@@ -228,6 +231,7 @@ def tile_iag_pb_v_kernel(tc, T1, T2, Wf, bn_g, bn_b, z, mu, rstd, grad_out, out)
             for j, acc in vector_banks:
                 empty(c - 1, j, acc, nc.vector.tensor_copy)
             vector_banks = []
+            scalar_banks = SCALAR_BANKS if c + 1 < CHUNKS else TILES // 2
             for j in range(TILES):
                 rows = slice(j * P, (j + 1) * P)
                 acc = psum.tile([P, EMB], F32, tag="f32_bank")
@@ -237,7 +241,7 @@ def tile_iag_pb_v_kernel(tc, T1, T2, Wf, bn_g, bn_b, z, mu, rstd, grad_out, out)
                     rhs=w_codes[:].bitcast(E4M3_X4), rhs_scale=w_scales[:],
                     start=True, stop=True,
                 )
-                if j < SCALAR_BANKS:
+                if j < scalar_banks:
                     empty(c, j, acc, nc.scalar.copy)
                 else:
                     vector_banks.append((j, acc))

@@ -22,7 +22,7 @@ CHUNK = TILES * P
 CHUNKS = ROWS // CHUNK
 RUN = 4
 VECTOR_PLANES = 1
-VECTOR_BANKS = 1
+VECTOR_BANKS = 0
 SCALAR_PLANES = PACK - VECTOR_PLANES
 SCALAR_BANKS = TILES - VECTOR_BANKS
 AHEAD = 2
@@ -63,6 +63,12 @@ def tile_iag_pb_v_kernel(tc, T1, T2, Wf, bn_g, bn_b, z, mu, rstd, grad_out, out)
         nc.sync.dma_start(out=rows_f32[PACK : 2 * PACK, :], in_=rstd.rearrange("(t p) -> t p", p=P))
         nc.sync.dma_start(out=rows_bf16[0:PACK, :], in_=bn_g.rearrange("(t p) -> t p", p=P))
         nc.sync.dma_start(out=rows_bf16[PACK : 2 * PACK, :], in_=bn_b.rearrange("(t p) -> t p", p=P))
+        w_planes = const.tile([P, PACK, EMB], BF16)
+        nc.sync.dma_start(out=w_planes[:], in_=Wf.rearrange("(t p) c -> p t c", p=P)[:, :, 0:EMB])
+
+        warm = const.tile([P, 1], F32)
+        nc.gpsimd.memset(warm[:], 0.0)
+        nc.scalar.activation(out=warm[:], in_=warm[:], func=ACT.Identity)
 
         z_in = []
         g_in = []
@@ -74,8 +80,6 @@ def tile_iag_pb_v_kernel(tc, T1, T2, Wf, bn_g, bn_b, z, mu, rstd, grad_out, out)
                 columns = slice(k * EMB // pieces, (k + 1) * EMB // pieces)
                 nc.sync.dma_start(out=z_in[c][:, :, columns], in_=z_chunks[c][:, :, columns])
                 nc.sync.dma_start(out=g_in[c][:, :, columns], in_=g_chunks[c][:, :, columns])
-        w_planes = const.tile([P, PACK, EMB], BF16)
-        nc.sync.dma_start(out=w_planes[:], in_=Wf.rearrange("(t p) c -> p t c", p=P)[:, :, 0:EMB])
 
         ident_f32 = const.tile([P, P], F32)
         ident_bf16 = const.tile([P, P], BF16)
@@ -86,12 +90,9 @@ def tile_iag_pb_v_kernel(tc, T1, T2, Wf, bn_g, bn_b, z, mu, rstd, grad_out, out)
         cols_bf16 = psum.tile([P, P], BF16, tag="bf16_bank", bufs=3)
         nc.tensor.transpose(out=cols_f32[:], in_=rows_f32[:], identity=ident_f32[:])
         nc.tensor.transpose(out=cols_bf16[:], in_=rows_bf16[:], identity=ident_bf16[:])
-        saved = const.tile([P, 2 * PACK], F32)
+        mean = cols_f32[:, 0:PACK]
+        inv_std = cols_f32[:, PACK : 2 * PACK]
         affine = const.tile([P, 2 * PACK], F32)
-        nc.vector.tensor_copy(out=affine[:], in_=cols_bf16[:, 0 : 2 * PACK])
-        nc.scalar.copy(out=saved[:], in_=cols_f32[:, 0 : 2 * PACK])
-        mean = saved[:, 0:PACK]
-        inv_std = saved[:, PACK : 2 * PACK]
         gamma = affine[:, 0:PACK]
         beta = affine[:, PACK : 2 * PACK]
 
@@ -100,8 +101,13 @@ def tile_iag_pb_v_kernel(tc, T1, T2, Wf, bn_g, bn_b, z, mu, rstd, grad_out, out)
         xs_bias = const.tile([P, PACK], F32)
         gain = const.tile([P, PACK], F32)
         threshold = const.tile([P, PACK], F32)
+        w_grouped = const.tile([P, EMB, PACK], BF16, align_bytes=64)
+        w_codes = const.tile([P, EMB], U32, align_bytes=64)
+        w_scales = const.tile([P, EMB], U8, align_bytes=64)
+
         nc.vector.tensor_scalar(
-            out=half_sign[:], in0=gamma, scalar1=0.0, scalar2=0.5, op0=ALU.is_ge, op1=ALU.subtract
+            out=half_sign[:], in0=cols_bf16[:, 0:PACK], scalar1=0.0, scalar2=0.5,
+            op0=ALU.is_ge, op1=ALU.subtract,
         )
         nc.vector.scalar_tensor_tensor(
             out=xs_scale[:], in0=half_sign[:], scalar=2.0, in1=inv_std, op0=ALU.mult, op1=ALU.mult
@@ -109,13 +115,19 @@ def tile_iag_pb_v_kernel(tc, T1, T2, Wf, bn_g, bn_b, z, mu, rstd, grad_out, out)
         nc.vector.scalar_tensor_tensor(
             out=xs_bias[:], in0=mean, scalar=-1.0, in1=xs_scale[:], op0=ALU.mult, op1=ALU.mult
         )
+        nc.vector.tensor_copy(out=affine[:], in_=cols_bf16[:, 0 : 2 * PACK])
         nc.vector.tensor_mul(out=gain[:], in0=inv_std, in1=gamma)
+        nc.vector.tensor_copy(out=as_words(w_grouped[:]), in_=by_word(w_planes[:]))
         nc.vector.scalar_tensor_tensor(
             out=threshold[:], in0=half_sign[:], scalar=2.0, in1=gamma, op0=ALU.mult, op1=ALU.mult
         )
         nc.vector.reciprocal(out=threshold[:], in_=threshold[:])
         nc.vector.scalar_tensor_tensor(
             out=threshold[:], in0=beta, scalar=-1.0, in1=threshold[:], op0=ALU.mult, op1=ALU.mult
+        )
+        nc.vector.quantize_mx(
+            out=w_codes[:].bitcast(E4M3_X4), scales=w_scales[:],
+            in_=w_grouped[:].rearrange("p c t -> p (c t)"),
         )
 
         xs = [resident.tile([P, PACK, CHUNK], F32, name="xs") for c in range(CHUNKS)]
@@ -153,21 +165,8 @@ def tile_iag_pb_v_kernel(tc, T1, T2, Wf, bn_g, bn_b, z, mu, rstd, grad_out, out)
                 op0=ALU.mult, op1=ALU.mult, accum_out=sum_gx[:, t, c : c + 1],
             )
 
-        w_grouped = const.tile([P, EMB, PACK], BF16, align_bytes=64)
-        w_codes = const.tile([P, EMB], U32, align_bytes=64)
-        w_scales = const.tile([P, EMB], U8, align_bytes=64)
-
-        def quantise_weights():
-            nc.scalar.copy(out=as_words(w_grouped[:]), in_=by_word(w_planes[:]))
-            nc.vector.quantize_mx(
-                out=w_codes[:].bitcast(E4M3_X4), scales=w_scales[:],
-                in_=w_grouped[:].rearrange("p c t -> p (c t)"),
-            )
-
         steps = [(c, t) for c in range(CHUNKS) for t in range(PACK)]
         for i in range(len(steps)):
-            if steps[i] == (CHUNKS - 1, 0):
-                quantise_weights()
             mask_gradient(*steps[i])
             if i > 0:
                 correlate(*steps[i - 1])

@@ -20,11 +20,11 @@ ROWS = 4 * 640
 TILES = 4
 CHUNK = TILES * P
 CHUNKS = ROWS // CHUNK
+PAIR = 2
+FUSED = 3
 RUN = 4
-VECTOR_PLANES = 1
-VECTOR_BANKS = 0
-SCALAR_PLANES = PACK - VECTOR_PLANES
-SCALAR_BANKS = TILES - VECTOR_BANKS
+STEEP = 2.0**60
+FLOOR = 200.0
 AHEAD = 2
 
 FLOPS = 2 * ROWS * EMB * EMB
@@ -37,6 +37,10 @@ def by_word(planes):
 
 def as_words(grouped):
     return grouped.rearrange("p (c i) t -> p c t i", i=RUN)
+
+
+def vector_banks(c):
+    return TILES // 2 if c == CHUNKS - 1 else 1
 
 
 def tile_iag_pb_v_kernel(tc, T1, T2, Wf, bn_g, bn_b, z, mu, rstd, grad_out, out):
@@ -52,8 +56,9 @@ def tile_iag_pb_v_kernel(tc, T1, T2, Wf, bn_g, bn_b, z, mu, rstd, grad_out, out)
         resident = ctx.enter_context(tc.tile_pool(name="resident", bufs=CHUNKS))
         stream = ctx.enter_context(tc.tile_pool(name="stream", bufs=4))
         stage = ctx.enter_context(tc.tile_pool(name="stage", bufs=2))
+        means = ctx.enter_context(tc.tile_pool(name="means", bufs=AHEAD + 1))
         outgoing = ctx.enter_context(tc.tile_pool(name="outgoing", bufs=2 * TILES))
-        psum = ctx.enter_context(tc.psum_pool(name="psum", bufs=5))
+        psum = ctx.enter_context(tc.psum_pool(name="psum", bufs=8))
 
         rows_f32 = const.tile([P, P], F32)
         rows_bf16 = const.tile([P, P], BF16)
@@ -63,12 +68,10 @@ def tile_iag_pb_v_kernel(tc, T1, T2, Wf, bn_g, bn_b, z, mu, rstd, grad_out, out)
         nc.sync.dma_start(out=rows_f32[PACK : 2 * PACK, :], in_=rstd.rearrange("(t p) -> t p", p=P))
         nc.sync.dma_start(out=rows_bf16[0:PACK, :], in_=bn_g.rearrange("(t p) -> t p", p=P))
         nc.sync.dma_start(out=rows_bf16[PACK : 2 * PACK, :], in_=bn_b.rearrange("(t p) -> t p", p=P))
-        w_planes = const.tile([P, PACK, EMB], BF16)
-        nc.sync.dma_start(out=w_planes[:], in_=Wf.rearrange("(t p) c -> p t c", p=P)[:, :, 0:EMB])
 
         warm = const.tile([P, 1], F32)
         nc.gpsimd.memset(warm[:], 0.0)
-        nc.scalar.activation(out=warm[:], in_=warm[:], func=ACT.Identity)
+        nc.scalar.activation(out=warm[:], in_=warm[:], func=ACT.Sigmoid)
 
         z_in = []
         g_in = []
@@ -80,124 +83,160 @@ def tile_iag_pb_v_kernel(tc, T1, T2, Wf, bn_g, bn_b, z, mu, rstd, grad_out, out)
                 columns = slice(k * EMB // pieces, (k + 1) * EMB // pieces)
                 nc.sync.dma_start(out=z_in[c][:, :, columns], in_=z_chunks[c][:, :, columns])
                 nc.sync.dma_start(out=g_in[c][:, :, columns], in_=g_chunks[c][:, :, columns])
+        w_planes = const.tile([P, PACK, EMB], BF16)
+        nc.sync.dma_start(out=w_planes[:], in_=Wf.rearrange("(t p) c -> p t c", p=P)[:, :, 0:EMB])
 
         ident_f32 = const.tile([P, P], F32)
         ident_bf16 = const.tile([P, P], BF16)
         make_identity(nc, ident_f32[:])
         make_identity(nc, ident_bf16[:])
+        w_grouped = const.tile([P, EMB, PACK], BF16, align_bytes=64)
+        nc.gpsimd.tensor_scalar(
+            out=as_words(w_grouped[:]), in0=by_word(w_planes[:]), scalar1=1.0, scalar2=0.0,
+            op0=ALU.mult, op1=ALU.add,
+        )
 
-        cols_f32 = psum.tile([P, P], F32, tag="f32_bank")
-        cols_bf16 = psum.tile([P, P], BF16, tag="bf16_bank", bufs=3)
+        cols_f32 = psum.tile([P, P], F32, tag="bank")
+        cols_bf16 = psum.tile([P, P], BF16, tag="bank")
         nc.tensor.transpose(out=cols_f32[:], in_=rows_f32[:], identity=ident_f32[:])
         nc.tensor.transpose(out=cols_bf16[:], in_=rows_bf16[:], identity=ident_bf16[:])
-        mean = cols_f32[:, 0:PACK]
-        inv_std = cols_f32[:, PACK : 2 * PACK]
-        affine = const.tile([P, 2 * PACK], F32)
-        gamma = affine[:, 0:PACK]
-        beta = affine[:, PACK : 2 * PACK]
-
-        half_sign = const.tile([P, PACK], F32)
-        xs_scale = const.tile([P, PACK], F32)
-        xs_bias = const.tile([P, PACK], F32)
         gain = const.tile([P, PACK], F32)
-        threshold = const.tile([P, PACK], F32)
-        w_grouped = const.tile([P, EMB, PACK], BF16, align_bytes=64)
+        stats = const.tile([P, 2 * PACK], F32)
+        mean = stats[:, 0:PACK]
+        inv_std = stats[:, PACK : 2 * PACK]
+        gamma_beta = const.tile([P, 2 * PACK], F32)
+        neg_mean = const.tile([P, PACK], F32)
+        mask_scale = const.tile([P, PACK], F32)
+        mask_bias = const.tile([P, PACK], F32)
+        slope_factor = const.tile([P, PACK], F32)
+
+        nc.vector.tensor_copy(out=stats[:], in_=cols_f32[:, 0 : 2 * PACK])
+        nc.vector.tensor_copy(out=gamma_beta[:], in_=cols_bf16[:, 0 : 2 * PACK])
+        nc.vector.tensor_mul(out=gain[:], in0=inv_std, in1=gamma_beta[:, 0:PACK])
+        nc.vector.tensor_scalar_mul(out=neg_mean[:], in0=mean, scalar1=-1.0)
+        nc.vector.tensor_scalar_mul(out=mask_scale[:], in0=gain[:], scalar1=STEEP)
+        nc.vector.tensor_mul(out=mask_bias[:], in0=neg_mean[:], in1=gain[:])
+        nc.vector.tensor_add(out=mask_bias[:], in0=mask_bias[:], in1=gamma_beta[:, PACK : 2 * PACK])
+        nc.vector.tensor_scalar(
+            out=mask_bias[:], in0=mask_bias[:], scalar1=STEEP, scalar2=-FLOOR, op0=ALU.mult, op1=ALU.add
+        )
+        nc.vector.scalar_tensor_tensor(
+            out=slope_factor[:], in0=inv_std, scalar=-1.0 / ROWS, in1=inv_std, op0=ALU.mult, op1=ALU.mult
+        )
+        nc.vector.tensor_mul(out=slope_factor[:, 0:FUSED], in0=slope_factor[:, 0:FUSED], in1=gain[:, 0:FUSED])
+
+        gma = [resident.tile([P, PACK, CHUNK], F32, name="gma") for c in range(CHUNKS)]
+        sums = const.tile([P, 2, PACK, CHUNKS], F32)
+
+        def transpose_z(c, t):
+            bank = psum.tile([P, CHUNK], F32, tag="bank")
+            for j in range(TILES):
+                nc.tensor.transpose(
+                    out=bank[:, j * P : (j + 1) * P],
+                    in_=z_in[c][:, j, t * P : (t + 1) * P], identity=ident_f32[:],
+                )
+            return bank
+
+        def transpose_pair(c, planes):
+            z_t = [transpose_z(c, t) for t in planes]
+            g_t = psum.tile([P, PAIR, CHUNK], BF16, tag="bank")
+            for k in range(PAIR):
+                for j in range(TILES):
+                    nc.tensor.transpose(
+                        out=g_t[:, k, j * P : (j + 1) * P],
+                        in_=g_in[c][:, j, planes[k] * P : (planes[k] + 1) * P], identity=ident_bf16[:],
+                    )
+            return z_t, g_t
+
+        def make_mask(z_t, planes):
+            mask = stream.tile([P, PAIR, CHUNK], BF16)
+            for k in range(PAIR):
+                t = planes[k]
+                nc.scalar.activation(
+                    out=mask[:, k, :], in_=z_t[k][:], func=ACT.Sigmoid,
+                    scale=mask_scale[:, t : t + 1], bias=mask_bias[:, t : t + 1],
+                )
+            return mask
+
+        def apply_mask(c, planes, mask, g_t):
+            gm = stream.tile([P, PAIR, CHUNK], BF16)
+            plain = PAIR - 1 if FUSED in planes else PAIR
+            nc.vector.tensor_tensor(
+                out=gm[:, 0:plain, :], in0=mask[:, 0:plain, :], in1=g_t[:, 0:plain, :], op=ALU.mult
+            )
+            if FUSED in planes:
+                nc.vector.scalar_tensor_tensor(
+                    out=gma[c][:, FUSED, :], in0=mask[:, plain, :], scalar=gain[:, FUSED : FUSED + 1],
+                    in1=g_t[:, plain, :], op0=ALU.mult, op1=ALU.mult,
+                    accum_out=sums[:, 0, FUSED, c : c + 1],
+                )
+            return [gma[c][:, t, :] if t == FUSED else gm[:, k, :] for k, t in enumerate(planes)]
+
+        def apply_gain(c, planes, masked):
+            for k, t in enumerate(planes):
+                if t != FUSED:
+                    nc.scalar.activation(
+                        out=gma[c][:, t, :], in_=masked[k], func=ACT.Identity,
+                        scale=gain[:, t : t + 1], accum_out=sums[:, 0, t, c : c + 1],
+                    )
+
+        def correlate(k, c, planes, z_t, masked):
+            t = planes[k]
+            product = stream.tile([P, CHUNK], F32)
+            nc.vector.scalar_tensor_tensor(
+                out=product[:], in0=z_t[k][:], scalar=mean[:, t : t + 1], in1=masked[k],
+                op0=ALU.subtract, op1=ALU.mult, accum_out=sums[:, 1, t, c : c + 1],
+            )
+
+        steps = [(c, (k, k + 1)) for c in range(CHUNKS) for k in range(0, PACK, PAIR)]
+        before = None
+        for c, planes in steps:
+            z_t, g_t = transpose_pair(c, planes)
+            mask = make_mask(z_t, planes)
+            masked = apply_mask(c, planes, mask, g_t)
+            if before is not None:
+                apply_gain(before[0], before[1], before[3])
+                correlate(1, *before)
+            before = (c, planes, z_t, masked)
+            correlate(0, *before)
+        apply_gain(before[0], before[1], before[3])
+
+        slope = const.tile([P, PACK], F32)
+        shift = const.tile([P, PACK], F32)
+
+        def finish_planes(first):
+            pair = slice(first, first + PAIR)
+            totals = const.tile([P, 2, PAIR], F32, name="totals%d" % first)
+            part = const.tile([P, PAIR], F32, name="part%d" % first)
+            nc.vector.reduce_sum(out=totals[:], in_=sums[:, :, pair, :], axis=AXIS.X)
+            nc.vector.tensor_mul(out=slope[:, pair], in0=totals[:, 1, :], in1=slope_factor[:, pair])
+            nc.vector.tensor_mul(out=part[:], in0=slope[:, pair], in1=neg_mean[:, pair])
+            nc.vector.scalar_tensor_tensor(
+                out=shift[:, pair], in0=totals[:, 0, :], scalar=-1.0 / ROWS, in1=part[:],
+                op0=ALU.mult, op1=ALU.add,
+            )
+
+        finish_planes(0)
+        correlate(1, *before)
+        finish_planes(PAIR)
+
         w_codes = const.tile([P, EMB], U32, align_bytes=64)
         w_scales = const.tile([P, EMB], U8, align_bytes=64)
 
-        nc.vector.tensor_scalar(
-            out=half_sign[:], in0=cols_bf16[:, 0:PACK], scalar1=0.0, scalar2=0.5,
-            op0=ALU.is_ge, op1=ALU.subtract,
-        )
-        nc.vector.scalar_tensor_tensor(
-            out=xs_scale[:], in0=half_sign[:], scalar=2.0, in1=inv_std, op0=ALU.mult, op1=ALU.mult
-        )
-        nc.vector.scalar_tensor_tensor(
-            out=xs_bias[:], in0=mean, scalar=-1.0, in1=xs_scale[:], op0=ALU.mult, op1=ALU.mult
-        )
-        nc.vector.tensor_copy(out=affine[:], in_=cols_bf16[:, 0 : 2 * PACK])
-        nc.vector.tensor_mul(out=gain[:], in0=inv_std, in1=gamma)
-        nc.vector.tensor_copy(out=as_words(w_grouped[:]), in_=by_word(w_planes[:]))
-        nc.vector.scalar_tensor_tensor(
-            out=threshold[:], in0=half_sign[:], scalar=2.0, in1=gamma, op0=ALU.mult, op1=ALU.mult
-        )
-        nc.vector.reciprocal(out=threshold[:], in_=threshold[:])
-        nc.vector.scalar_tensor_tensor(
-            out=threshold[:], in0=beta, scalar=-1.0, in1=threshold[:], op0=ALU.mult, op1=ALU.mult
-        )
-        nc.vector.quantize_mx(
-            out=w_codes[:].bitcast(E4M3_X4), scales=w_scales[:],
-            in_=w_grouped[:].rearrange("p c t -> p (c t)"),
-        )
-
-        xs = [resident.tile([P, PACK, CHUNK], F32, name="xs") for c in range(CHUNKS)]
-        gma = [resident.tile([P, PACK, CHUNK], F32, name="gma") for c in range(CHUNKS)]
-        sum_g = const.tile([P, PACK, CHUNKS], F32)
-        sum_gx = const.tile([P, PACK, CHUNKS], F32)
-
-        def mask_gradient(c, t):
-            channels = slice(t * P, (t + 1) * P)
-            z_t = psum.tile([P, CHUNK], F32, tag="f32_bank")
-            g_t = psum.tile([P, CHUNK], BF16, tag="bf16_bank", bufs=3)
-            for j in range(TILES):
-                nc.tensor.transpose(
-                    out=z_t[:, j * P : (j + 1) * P], in_=z_in[c][:, j, channels], identity=ident_f32[:]
-                )
-            for j in range(TILES):
-                nc.tensor.transpose(
-                    out=g_t[:, j * P : (j + 1) * P], in_=g_in[c][:, j, channels], identity=ident_bf16[:]
-                )
-            nc.scalar.activation(
-                out=xs[c][:, t, :], in_=z_t[:], func=ACT.Identity,
-                scale=xs_scale[:, t : t + 1], bias=xs_bias[:, t : t + 1],
-            )
-            g_scaled = stream.tile([P, CHUNK], F32)
-            nc.scalar.activation(out=g_scaled[:], in_=g_t[:], func=ACT.Identity, scale=gain[:, t : t + 1])
-            nc.vector.scalar_tensor_tensor(
-                out=gma[c][:, t, :], in0=xs[c][:, t, :], scalar=threshold[:, t : t + 1], in1=g_scaled[:],
-                op0=ALU.is_gt, op1=ALU.mult, accum_out=sum_g[:, t, c : c + 1],
-            )
-
-        def correlate(c, t):
-            product = stream.tile([P, CHUNK], F32)
-            nc.vector.scalar_tensor_tensor(
-                out=product[:], in0=gma[c][:, t, :], scalar=1.0, in1=xs[c][:, t, :],
-                op0=ALU.mult, op1=ALU.mult, accum_out=sum_gx[:, t, c : c + 1],
-            )
-
-        steps = [(c, t) for c in range(CHUNKS) for t in range(PACK)]
-        for i in range(len(steps)):
-            mask_gradient(*steps[i])
-            if i > 0:
-                correlate(*steps[i - 1])
-        correlate(*steps[-1])
-
-        shift = [const.tile([P, 1], F32, name="shift%d" % t) for t in range(PACK)]
-        slope = [const.tile([P, 1], F32, name="slope%d" % t) for t in range(PACK)]
-
-        def finish_plane(t):
-            for sums, scalar in ((sum_g, shift[t]), (sum_gx, slope[t])):
-                if t < SCALAR_PLANES:
-                    scaled = stream.tile([P, CHUNKS], F32)
-                    nc.scalar.activation(
-                        out=scaled[:], in_=sums[:, t, :], func=ACT.Identity,
-                        scale=-1.0 / ROWS, accum_out=scalar[:],
-                    )
-                else:
-                    total = stream.tile([P, 1], F32)
-                    nc.vector.reduce_sum(out=total[:], in_=sums[:, t, :], axis=AXIS.X)
-                    nc.vector.tensor_scalar_mul(out=scalar[:], in0=total[:], scalar1=-1.0 / ROWS)
+        terms = [means.tile([P, PACK, CHUNK], F32, name="terms") for c in range(AHEAD)]
 
         def means_term(c, t):
-            if t < SCALAR_PLANES:
-                nc.scalar.activation(
-                    out=xs[c][:, t, :], in_=xs[c][:, t, :], func=ACT.Identity,
-                    scale=slope[t][:], bias=shift[t][:],
+            bank = transpose_z(c, t)
+            term = terms[c][:, t, :]
+            if c == 0 and t == PACK - 1:
+                nc.vector.tensor_scalar(
+                    out=term, in0=bank[:], scalar1=slope[:, t : t + 1], scalar2=shift[:, t : t + 1],
+                    op0=ALU.mult, op1=ALU.add,
                 )
             else:
-                nc.vector.tensor_scalar(
-                    out=xs[c][:, t, :], in0=xs[c][:, t, :], scalar1=slope[t][:],
-                    scalar2=shift[t][:], op0=ALU.mult, op1=ALU.add,
+                nc.scalar.activation(
+                    out=term, in_=bank[:], func=ACT.Identity,
+                    scale=slope[:, t : t + 1], bias=shift[:, t : t + 1],
                 )
 
         def empty(c, j, acc, copy):
@@ -205,44 +244,50 @@ def tile_iag_pb_v_kernel(tc, T1, T2, Wf, bn_g, bn_b, z, mu, rstd, grad_out, out)
             copy(out=result[:], in_=acc[:])
             nc.sync.dma_start(out=out_tiles[c, j], in_=result[:])
 
-        for t in range(PACK):
-            finish_plane(t)
-            means_term(0, t)
-        for c in range(1, AHEAD):
+        for c in range(AHEAD):
             for t in range(PACK):
                 means_term(c, t)
-
-        vector_banks = []
+        for_vector = []
         for c in range(CHUNKS):
+            pieces = 2 if c == CHUNKS - 1 else 1
+            spans = [slice(k * CHUNK // pieces, (k + 1) * CHUNK // pieces) for k in range(pieces)]
             dz_grouped = stage.tile([P, CHUNK, PACK], BF16, align_bytes=64)
-            nc.vector.tensor_tensor(
-                out=as_words(dz_grouped[:]), in0=by_word(gma[c][:]), in1=by_word(xs[c][:]), op=ALU.add
-            )
+            for rows in spans:
+                nc.vector.tensor_tensor(
+                    out=as_words(dz_grouped[:, rows, :]), in0=by_word(gma[c][:, :, rows]),
+                    in1=by_word(terms[c][:, :, rows]), op=ALU.add,
+                )
             if c + AHEAD < CHUNKS:
+                terms.append(means.tile([P, PACK, CHUNK], F32, name="terms"))
                 for t in range(PACK):
                     means_term(c + AHEAD, t)
+            if c == 0:
+                nc.vector.quantize_mx(
+                    out=w_codes[:].bitcast(E4M3_X4), scales=w_scales[:],
+                    in_=w_grouped[:].rearrange("p c t -> p (c t)"),
+                )
+            for j, acc in for_vector:
+                empty(c - 1, j, acc, nc.vector.tensor_copy)
             dz_codes = stage.tile([P, CHUNK], U32, align_bytes=64)
             dz_scales = stage.tile([P, CHUNK], U8, align_bytes=64)
-            nc.vector.quantize_mx(
-                out=dz_codes[:].bitcast(E5M2_X4), scales=dz_scales[:],
-                in_=dz_grouped[:].rearrange("p w t -> p (w t)"),
-            )
-            for j, acc in vector_banks:
-                empty(c - 1, j, acc, nc.vector.tensor_copy)
-            vector_banks = []
-            scalar_banks = SCALAR_BANKS if c + 1 < CHUNKS else TILES // 2
+            for rows in spans:
+                nc.vector.quantize_mx(
+                    out=dz_codes[:, rows].bitcast(E5M2_X4), scales=dz_scales[:, rows],
+                    in_=dz_grouped[:, rows, :].rearrange("p w t -> p (w t)"),
+                )
+            for_vector = []
             for j in range(TILES):
                 rows = slice(j * P, (j + 1) * P)
-                acc = psum.tile([P, EMB], F32, tag="f32_bank")
+                acc = psum.tile([P, EMB], F32, tag="bank")
                 nc.tensor.matmul_mx(
                     out=acc[:],
                     lhsT=dz_codes[:, rows].bitcast(E5M2_X4), lhsT_scale=dz_scales[:, rows],
                     rhs=w_codes[:].bitcast(E4M3_X4), rhs_scale=w_scales[:],
                     start=True, stop=True,
                 )
-                if j < scalar_banks:
+                if j < TILES - vector_banks(c):
                     empty(c, j, acc, nc.scalar.copy)
                 else:
-                    vector_banks.append((j, acc))
-        for j, acc in vector_banks:
+                    for_vector.append((j, acc))
+        for j, acc in for_vector:
             empty(CHUNKS - 1, j, acc, nc.vector.tensor_copy)

@@ -17,9 +17,10 @@ P = 128
 PACK = 4
 EMB = 512
 ROWS = 4 * 640
-TILES = 4
-CHUNK = TILES * P
-CHUNKS = ROWS // CHUNK
+TILES = (2, 4, 4, 4, 4, 2)
+CHUNKS = len(TILES)
+STARTS = [P * sum(TILES[:c]) for c in range(CHUNKS)]
+CHUNK = P * max(TILES)
 PAIR = 2
 FUSED = 3
 RUN = 4
@@ -39,16 +40,15 @@ def as_words(grouped):
     return grouped.rearrange("p (c i) t -> p c t i", i=RUN)
 
 
-def vector_banks(c):
-    return TILES // 2 if c == CHUNKS - 1 else 1
+VECTOR_BANKS = (0, 1, 1, 1, 0, 1)
 
 
 def tile_iag_pb_v_kernel(tc, T1, T2, Wf, bn_g, bn_b, z, mu, rstd, grad_out, out):
     nc = tc.nc
 
-    z_chunks = z.flatten_outer_dims().rearrange("(c p j) o -> c p j o", p=P, j=TILES)
-    g_chunks = grad_out.flatten_outer_dims().rearrange("(c p j) o -> c p j o", p=P, j=TILES)
-    out_tiles = out.flatten_outer_dims().rearrange("(c p j) o -> c j p o", p=P, j=TILES)
+    def in_chunk(rows, c, pattern):
+        part = rows.flatten_outer_dims()[STARTS[c] : STARTS[c] + P * TILES[c], :]
+        return part.rearrange(pattern, p=P, j=TILES[c])
 
     with ExitStack() as ctx:
         ctx.enter_context(tc.manual_schedule())
@@ -57,7 +57,7 @@ def tile_iag_pb_v_kernel(tc, T1, T2, Wf, bn_g, bn_b, z, mu, rstd, grad_out, out)
         stream = ctx.enter_context(tc.tile_pool(name="stream", bufs=4))
         stage = ctx.enter_context(tc.tile_pool(name="stage", bufs=2))
         means = ctx.enter_context(tc.tile_pool(name="means", bufs=AHEAD + 1))
-        outgoing = ctx.enter_context(tc.tile_pool(name="outgoing", bufs=2 * TILES))
+        outgoing = ctx.enter_context(tc.tile_pool(name="outgoing", bufs=2 * max(TILES)))
         psum = ctx.enter_context(tc.psum_pool(name="psum", bufs=8))
 
         rows_f32 = const.tile([P, P], F32)
@@ -76,13 +76,10 @@ def tile_iag_pb_v_kernel(tc, T1, T2, Wf, bn_g, bn_b, z, mu, rstd, grad_out, out)
         z_in = []
         g_in = []
         for c in range(CHUNKS):
-            z_in.append(resident.tile([P, TILES, EMB], F32, name="z_in"))
-            g_in.append(resident.tile([P, TILES, EMB], BF16, name="g_in"))
-            pieces = 2 if c == 0 else 1
-            for k in range(pieces):
-                columns = slice(k * EMB // pieces, (k + 1) * EMB // pieces)
-                nc.sync.dma_start(out=z_in[c][:, :, columns], in_=z_chunks[c][:, :, columns])
-                nc.sync.dma_start(out=g_in[c][:, :, columns], in_=g_chunks[c][:, :, columns])
+            z_in.append(resident.tile([P, max(TILES), EMB], F32, name="z_in"))
+            g_in.append(resident.tile([P, max(TILES), EMB], BF16, name="g_in"))
+            nc.sync.dma_start(out=z_in[c][:, 0 : TILES[c], :], in_=in_chunk(z, c, "(p j) o -> p j o"))
+            nc.sync.dma_start(out=g_in[c][:, 0 : TILES[c], :], in_=in_chunk(grad_out, c, "(p j) o -> p j o"))
         w_planes = const.tile([P, PACK, EMB], BF16)
         nc.sync.dma_start(out=w_planes[:], in_=Wf.rearrange("(t p) c -> p t c", p=P)[:, :, 0:EMB])
 
@@ -104,79 +101,91 @@ def tile_iag_pb_v_kernel(tc, T1, T2, Wf, bn_g, bn_b, z, mu, rstd, grad_out, out)
         stats = const.tile([P, 2 * PACK], F32)
         mean = stats[:, 0:PACK]
         inv_std = stats[:, PACK : 2 * PACK]
-        gamma_beta = const.tile([P, 2 * PACK], F32)
+        gamma = const.tile([P, PACK], F32)
+        steep_beta = const.tile([P, PACK], F32)
         neg_mean = const.tile([P, PACK], F32)
         mask_scale = const.tile([P, PACK], F32)
         mask_bias = const.tile([P, PACK], F32)
         slope_factor = const.tile([P, PACK], F32)
+        shift_factor = const.tile([P, PACK], F32)
 
-        nc.vector.tensor_copy(out=stats[:], in_=cols_f32[:, 0 : 2 * PACK])
-        nc.vector.tensor_copy(out=gamma_beta[:], in_=cols_bf16[:, 0 : 2 * PACK])
-        nc.vector.tensor_mul(out=gain[:], in0=inv_std, in1=gamma_beta[:, 0:PACK])
-        nc.vector.tensor_scalar_mul(out=neg_mean[:], in0=mean, scalar1=-1.0)
-        nc.vector.tensor_scalar_mul(out=mask_scale[:], in0=gain[:], scalar1=STEEP)
-        nc.vector.tensor_mul(out=mask_bias[:], in0=neg_mean[:], in1=gain[:])
-        nc.vector.tensor_add(out=mask_bias[:], in0=mask_bias[:], in1=gamma_beta[:, PACK : 2 * PACK])
+        nc.vector.tensor_copy(out=gamma[:], in_=cols_bf16[:, 0:PACK])
         nc.vector.tensor_scalar(
-            out=mask_bias[:], in0=mask_bias[:], scalar1=STEEP, scalar2=-FLOOR, op0=ALU.mult, op1=ALU.add
+            out=steep_beta[:], in0=cols_bf16[:, PACK : 2 * PACK], scalar1=STEEP, scalar2=-FLOOR,
+            op0=ALU.mult, op1=ALU.add,
         )
+        nc.vector.scalar_tensor_tensor(
+            out=mask_scale[:], in0=cols_f32[:, PACK : 2 * PACK], scalar=STEEP, in1=gamma[:],
+            op0=ALU.mult, op1=ALU.mult,
+        )
+        nc.vector.tensor_copy(out=stats[:], in_=cols_f32[:, 0 : 2 * PACK])
+        nc.vector.scalar_tensor_tensor(
+            out=mask_bias[:], in0=cols_f32[:, 0:PACK], scalar=-1.0, in1=mask_scale[:],
+            op0=ALU.mult, op1=ALU.mult,
+        )
+        nc.vector.tensor_mul(out=gain[:], in0=inv_std, in1=gamma[:])
+        nc.vector.tensor_add(out=mask_bias[:], in0=mask_bias[:], in1=steep_beta[:])
+        nc.vector.tensor_scalar_mul(out=neg_mean[:], in0=mean, scalar1=-1.0)
         nc.vector.scalar_tensor_tensor(
             out=slope_factor[:], in0=inv_std, scalar=-1.0 / ROWS, in1=inv_std, op0=ALU.mult, op1=ALU.mult
         )
         nc.vector.tensor_mul(out=slope_factor[:, 0:FUSED], in0=slope_factor[:, 0:FUSED], in1=gain[:, 0:FUSED])
+        nc.vector.tensor_mul(out=shift_factor[:], in0=slope_factor[:], in1=neg_mean[:])
 
         gma = [resident.tile([P, PACK, CHUNK], F32, name="gma") for c in range(CHUNKS)]
         sums = const.tile([P, 2, PACK, CHUNKS], F32)
 
         def transpose_z(c, t):
             bank = psum.tile([P, CHUNK], F32, tag="bank")
-            for j in range(TILES):
+            for j in range(TILES[c]):
                 nc.tensor.transpose(
                     out=bank[:, j * P : (j + 1) * P],
                     in_=z_in[c][:, j, t * P : (t + 1) * P], identity=ident_f32[:],
                 )
-            return bank
+            return bank[:, 0 : P * TILES[c]]
 
         def transpose_pair(c, planes):
             z_t = [transpose_z(c, t) for t in planes]
             g_t = psum.tile([P, PAIR, CHUNK], BF16, tag="bank")
             for k in range(PAIR):
-                for j in range(TILES):
+                for j in range(TILES[c]):
                     nc.tensor.transpose(
                         out=g_t[:, k, j * P : (j + 1) * P],
                         in_=g_in[c][:, j, planes[k] * P : (planes[k] + 1) * P], identity=ident_bf16[:],
                     )
-            return z_t, g_t
+            return z_t, g_t[:, :, 0 : P * TILES[c]]
 
-        def make_mask(z_t, planes):
+        def make_mask(c, planes, z_t):
             mask = stream.tile([P, PAIR, CHUNK], BF16)
+            mask = mask[:, :, 0 : P * TILES[c]]
             for k in range(PAIR):
                 t = planes[k]
                 nc.scalar.activation(
-                    out=mask[:, k, :], in_=z_t[k][:], func=ACT.Sigmoid,
+                    out=mask[:, k, :], in_=z_t[k], func=ACT.Sigmoid,
                     scale=mask_scale[:, t : t + 1], bias=mask_bias[:, t : t + 1],
                 )
             return mask
 
         def apply_mask(c, planes, mask, g_t):
+            rows = slice(0, P * TILES[c])
             gm = stream.tile([P, PAIR, CHUNK], BF16)
             plain = PAIR - 1 if FUSED in planes else PAIR
             nc.vector.tensor_tensor(
-                out=gm[:, 0:plain, :], in0=mask[:, 0:plain, :], in1=g_t[:, 0:plain, :], op=ALU.mult
+                out=gm[:, 0:plain, rows], in0=mask[:, 0:plain, :], in1=g_t[:, 0:plain, :], op=ALU.mult
             )
             if FUSED in planes:
                 nc.vector.scalar_tensor_tensor(
-                    out=gma[c][:, FUSED, :], in0=mask[:, plain, :], scalar=gain[:, FUSED : FUSED + 1],
+                    out=gma[c][:, FUSED, rows], in0=mask[:, plain, :], scalar=gain[:, FUSED : FUSED + 1],
                     in1=g_t[:, plain, :], op0=ALU.mult, op1=ALU.mult,
                     accum_out=sums[:, 0, FUSED, c : c + 1],
                 )
-            return [gma[c][:, t, :] if t == FUSED else gm[:, k, :] for k, t in enumerate(planes)]
+            return [gma[c][:, t, rows] if t == FUSED else gm[:, k, rows] for k, t in enumerate(planes)]
 
         def apply_gain(c, planes, masked):
             for k, t in enumerate(planes):
                 if t != FUSED:
                     nc.scalar.activation(
-                        out=gma[c][:, t, :], in_=masked[k], func=ACT.Identity,
+                        out=gma[c][:, t, 0 : P * TILES[c]], in_=masked[k], func=ACT.Identity,
                         scale=gain[:, t : t + 1], accum_out=sums[:, 0, t, c : c + 1],
                     )
 
@@ -184,41 +193,38 @@ def tile_iag_pb_v_kernel(tc, T1, T2, Wf, bn_g, bn_b, z, mu, rstd, grad_out, out)
             t = planes[k]
             product = stream.tile([P, CHUNK], F32)
             nc.vector.scalar_tensor_tensor(
-                out=product[:], in0=z_t[k][:], scalar=mean[:, t : t + 1], in1=masked[k],
+                out=product[:, 0 : P * TILES[c]], in0=z_t[k], scalar=mean[:, t : t + 1], in1=masked[k],
                 op0=ALU.subtract, op1=ALU.mult, accum_out=sums[:, 1, t, c : c + 1],
             )
 
         steps = [(c, (k, k + 1)) for c in range(CHUNKS) for k in range(0, PACK, PAIR)]
+        waiting = []
         before = None
-        for c, planes in steps:
+        for i, (c, planes) in enumerate(steps):
             z_t, g_t = transpose_pair(c, planes)
-            mask = make_mask(z_t, planes)
+            mask = make_mask(c, planes, z_t)
             masked = apply_mask(c, planes, mask, g_t)
+            if waiting and i + 1 < len(steps) - 1:
+                apply_gain(*waiting.pop(0))
+            waiting.append((c, planes, masked))
             if before is not None:
-                apply_gain(before[0], before[1], before[3])
                 correlate(1, *before)
             before = (c, planes, z_t, masked)
             correlate(0, *before)
-        apply_gain(before[0], before[1], before[3])
-
-        slope = const.tile([P, PACK], F32)
-        shift = const.tile([P, PACK], F32)
-
-        def finish_planes(first):
-            pair = slice(first, first + PAIR)
-            totals = const.tile([P, 2, PAIR], F32, name="totals%d" % first)
-            part = const.tile([P, PAIR], F32, name="part%d" % first)
-            nc.vector.reduce_sum(out=totals[:], in_=sums[:, :, pair, :], axis=AXIS.X)
-            nc.vector.tensor_mul(out=slope[:, pair], in0=totals[:, 1, :], in1=slope_factor[:, pair])
-            nc.vector.tensor_mul(out=part[:], in0=slope[:, pair], in1=neg_mean[:, pair])
-            nc.vector.scalar_tensor_tensor(
-                out=shift[:, pair], in0=totals[:, 0, :], scalar=-1.0 / ROWS, in1=part[:],
-                op0=ALU.mult, op1=ALU.add,
-            )
-
-        finish_planes(0)
+        while waiting:
+            apply_gain(*waiting.pop(0))
         correlate(1, *before)
-        finish_planes(PAIR)
+
+        totals = const.tile([P, 2, PACK], F32)
+        slope = const.tile([P, PACK], F32)
+        part = const.tile([P, PACK], F32)
+        shift = const.tile([P, PACK], F32)
+        nc.vector.reduce_sum(out=totals[:], in_=sums[:], axis=AXIS.X)
+        nc.vector.tensor_mul(out=part[:], in0=totals[:, 1, :], in1=shift_factor[:])
+        nc.vector.tensor_mul(out=slope[:], in0=totals[:, 1, :], in1=slope_factor[:])
+        nc.vector.scalar_tensor_tensor(
+            out=shift[:], in0=totals[:, 0, :], scalar=-1.0 / ROWS, in1=part[:], op0=ALU.mult, op1=ALU.add
+        )
 
         w_codes = const.tile([P, EMB], U32, align_bytes=64)
         w_scales = const.tile([P, EMB], U8, align_bytes=64)
@@ -227,30 +233,30 @@ def tile_iag_pb_v_kernel(tc, T1, T2, Wf, bn_g, bn_b, z, mu, rstd, grad_out, out)
 
         def means_term(c, t):
             bank = transpose_z(c, t)
-            term = terms[c][:, t, :]
-            if c == 0 and t == PACK - 1:
+            term = terms[c][:, t, 0 : P * TILES[c]]
+            if c == 0 and t >= PAIR:
                 nc.vector.tensor_scalar(
-                    out=term, in0=bank[:], scalar1=slope[:, t : t + 1], scalar2=shift[:, t : t + 1],
+                    out=term, in0=bank, scalar1=slope[:, t : t + 1], scalar2=shift[:, t : t + 1],
                     op0=ALU.mult, op1=ALU.add,
                 )
             else:
                 nc.scalar.activation(
-                    out=term, in_=bank[:], func=ACT.Identity,
+                    out=term, in_=bank, func=ACT.Identity,
                     scale=slope[:, t : t + 1], bias=shift[:, t : t + 1],
                 )
 
         def empty(c, j, acc, copy):
             result = outgoing.tile([P, EMB], F32)
             copy(out=result[:], in_=acc[:])
-            nc.sync.dma_start(out=out_tiles[c, j], in_=result[:])
+            nc.sync.dma_start(out=in_chunk(out, c, "(p j) o -> j p o")[j], in_=result[:])
 
         for c in range(AHEAD):
             for t in range(PACK):
                 means_term(c, t)
         for_vector = []
         for c in range(CHUNKS):
-            pieces = 2 if c == CHUNKS - 1 else 1
-            spans = [slice(k * CHUNK // pieces, (k + 1) * CHUNK // pieces) for k in range(pieces)]
+            bounds = (0, P, 2 * P) if c == CHUNKS - 1 else (0, P * TILES[c])
+            spans = [slice(a, b) for a, b in zip(bounds[:-1], bounds[1:])]
             dz_grouped = stage.tile([P, CHUNK, PACK], BF16, align_bytes=64)
             for rows in spans:
                 nc.vector.tensor_tensor(
@@ -276,7 +282,7 @@ def tile_iag_pb_v_kernel(tc, T1, T2, Wf, bn_g, bn_b, z, mu, rstd, grad_out, out)
                     in_=dz_grouped[:, rows, :].rearrange("p w t -> p (w t)"),
                 )
             for_vector = []
-            for j in range(TILES):
+            for j in range(TILES[c]):
                 rows = slice(j * P, (j + 1) * P)
                 acc = psum.tile([P, EMB], F32, tag="bank")
                 nc.tensor.matmul_mx(
@@ -285,7 +291,7 @@ def tile_iag_pb_v_kernel(tc, T1, T2, Wf, bn_g, bn_b, z, mu, rstd, grad_out, out)
                     rhs=w_codes[:].bitcast(E4M3_X4), rhs_scale=w_scales[:],
                     start=True, stop=True,
                 )
-                if j < TILES - vector_banks(c):
+                if j < TILES[c] - VECTOR_BANKS[c]:
                     empty(c, j, acc, nc.scalar.copy)
                 else:
                     for_vector.append((j, acc))

@@ -17,7 +17,7 @@ P = 128
 PACK = 4
 EMB = 512
 ROWS = 4 * 640
-TILES = (2, 4, 4, 4, 4, 2)
+TILES = (2, 3, 4, 4, 4, 3)
 CHUNKS = len(TILES)
 STARTS = [P * sum(TILES[:c]) for c in range(CHUNKS)]
 CHUNK = P * max(TILES)
@@ -40,7 +40,7 @@ def as_words(grouped):
     return grouped.rearrange("p (c i) t -> p c t i", i=RUN)
 
 
-VECTOR_BANKS = (0, 1, 1, 1, 0, 1)
+VECTOR_BANKS = (0, 0, 1, 0, 0, 2)
 
 
 def tile_iag_pb_v_kernel(tc, T1, T2, Wf, bn_g, bn_b, z, mu, rstd, grad_out, out):
@@ -57,7 +57,7 @@ def tile_iag_pb_v_kernel(tc, T1, T2, Wf, bn_g, bn_b, z, mu, rstd, grad_out, out)
         stream = ctx.enter_context(tc.tile_pool(name="stream", bufs=4))
         stage = ctx.enter_context(tc.tile_pool(name="stage", bufs=2))
         means = ctx.enter_context(tc.tile_pool(name="means", bufs=AHEAD + 1))
-        outgoing = ctx.enter_context(tc.tile_pool(name="outgoing", bufs=2 * max(TILES)))
+        outgoing = ctx.enter_context(tc.tile_pool(name="outgoing", bufs=3 * max(TILES)))
         psum = ctx.enter_context(tc.psum_pool(name="psum", bufs=8))
 
         rows_f32 = const.tile([P, P], F32)
@@ -197,7 +197,10 @@ def tile_iag_pb_v_kernel(tc, T1, T2, Wf, bn_g, bn_b, z, mu, rstd, grad_out, out)
                 op0=ALU.subtract, op1=ALU.mult, accum_out=sums[:, 1, t, c : c + 1],
             )
 
-        steps = [(c, (k, k + 1)) for c in range(CHUNKS) for k in range(0, PACK, PAIR)]
+        pairs = ((0, 1), (2, 3))
+        steps = [(c, planes) for c in range(CHUNKS) for planes in pairs]
+        late = slice(PAIR, PACK)
+        known = const.tile([P, PAIR], F32)
         waiting = []
         before = None
         for i, (c, planes) in enumerate(steps):
@@ -209,23 +212,56 @@ def tile_iag_pb_v_kernel(tc, T1, T2, Wf, bn_g, bn_b, z, mu, rstd, grad_out, out)
             waiting.append((c, planes, masked))
             if before is not None:
                 correlate(1, *before)
+            if i + 1 == len(steps):
+                nc.vector.reduce_sum(out=known[:], in_=sums[:, 1, late, 0 : CHUNKS - 1], axis=AXIS.X)
             before = (c, planes, z_t, masked)
             correlate(0, *before)
         while waiting:
             apply_gain(*waiting.pop(0))
-        correlate(1, *before)
 
-        totals = const.tile([P, 2, PACK], F32)
         slope = const.tile([P, PACK], F32)
-        part = const.tile([P, PACK], F32)
         shift = const.tile([P, PACK], F32)
-        nc.vector.reduce_sum(out=totals[:], in_=sums[:], axis=AXIS.X)
-        nc.vector.tensor_mul(out=part[:], in0=totals[:, 1, :], in1=shift_factor[:])
-        nc.vector.tensor_mul(out=slope[:], in0=totals[:, 1, :], in1=slope_factor[:])
+        minus_mean = const.tile([P, PAIR], F32)
+        total = const.tile([P, PAIR], F32)
+        part = const.tile([P, PAIR], F32)
+        base = const.tile([P, PAIR], F32)
+        nc.vector.tensor_mul(out=part[:], in0=known[:], in1=shift_factor[:, late])
+        nc.vector.reduce_sum(out=total[:], in_=sums[:, 0, late, :], axis=AXIS.X)
         nc.vector.scalar_tensor_tensor(
-            out=shift[:], in0=totals[:, 0, :], scalar=-1.0 / ROWS, in1=part[:], op0=ALU.mult, op1=ALU.add
+            out=base[:], in0=total[:], scalar=-1.0 / ROWS, in1=part[:], op0=ALU.mult, op1=ALU.add
         )
 
+        def finish(t):
+            last = sums[:, 1, t, CHUNKS - 1 : CHUNKS]
+            k = t - PAIR
+            nc.vector.scalar_tensor_tensor(
+                out=slope[:, t : t + 1], in0=last, scalar=known[:, k : k + 1],
+                in1=slope_factor[:, t : t + 1], op0=ALU.add, op1=ALU.mult,
+            )
+            nc.vector.scalar_tensor_tensor(
+                out=shift[:, t : t + 1], in0=last, scalar=shift_factor[:, t : t + 1],
+                in1=base[:, k : k + 1], op0=ALU.mult, op1=ALU.add,
+            )
+
+        finish(2)
+        correlate(1, *before)
+        for t in pairs[0]:
+            scaled = stream.tile([P, CHUNKS], F32)
+            nc.scalar.activation(
+                out=scaled[:], in_=sums[:, 0, t, :], func=ACT.Identity,
+                scale=-1.0 / ROWS, accum_out=minus_mean[:, t : t + 1],
+            )
+        for t in pairs[0]:
+            scaled = stream.tile([P, CHUNKS], F32)
+            nc.scalar.activation(
+                out=scaled[:], in_=sums[:, 1, t, :], func=ACT.Identity,
+                scale=slope_factor[:, t : t + 1], accum_out=slope[:, t : t + 1],
+            )
+        for t in pairs[0]:
+            nc.scalar.activation(
+                out=shift[:, t : t + 1], in_=slope[:, t : t + 1], func=ACT.Identity,
+                scale=neg_mean[:, t : t + 1], bias=minus_mean[:, t : t + 1],
+            )
         w_codes = const.tile([P, EMB], U32, align_bytes=64)
         w_scales = const.tile([P, EMB], U8, align_bytes=64)
 
@@ -250,13 +286,16 @@ def tile_iag_pb_v_kernel(tc, T1, T2, Wf, bn_g, bn_b, z, mu, rstd, grad_out, out)
             copy(out=result[:], in_=acc[:])
             nc.sync.dma_start(out=in_chunk(out, c, "(p j) o -> j p o")[j], in_=result[:])
 
-        for c in range(AHEAD):
-            for t in range(PACK):
-                means_term(c, t)
+        for t in range(PACK):
+            if t == 3:
+                finish(t)
+            means_term(0, t)
+        for t in range(PACK):
+            means_term(1, t)
         for_vector = []
         for c in range(CHUNKS):
-            bounds = (0, P, 2 * P) if c == CHUNKS - 1 else (0, P * TILES[c])
-            spans = [slice(a, b) for a, b in zip(bounds[:-1], bounds[1:])]
+            pieces = ((0, 2 * P), (2 * P, 3 * P)) if TILES[c] == 3 else ((0, P * TILES[c]),)
+            spans = [slice(a, b) for a, b in (pieces if c == CHUNKS - 1 else ((0, P * TILES[c]),))]
             dz_grouped = stage.tile([P, CHUNK, PACK], BF16, align_bytes=64)
             for rows in spans:
                 nc.vector.tensor_tensor(
@@ -276,7 +315,8 @@ def tile_iag_pb_v_kernel(tc, T1, T2, Wf, bn_g, bn_b, z, mu, rstd, grad_out, out)
                 empty(c - 1, j, acc, nc.vector.tensor_copy)
             dz_codes = stage.tile([P, CHUNK], U32, align_bytes=64)
             dz_scales = stage.tile([P, CHUNK], U8, align_bytes=64)
-            for rows in spans:
+            for a, b in pieces:
+                rows = slice(a, b)
                 nc.vector.quantize_mx(
                     out=dz_codes[:, rows].bitcast(E5M2_X4), scales=dz_scales[:, rows],
                     in_=dz_grouped[:, rows, :].rearrange("p w t -> p (w t)"),

@@ -22,6 +22,7 @@ CHUNKS = len(TILES)
 STARTS = [P * sum(TILES[:c]) for c in range(CHUNKS)]
 CHUNK = P * max(TILES)
 PAIR = 2
+GPSIMD_CHUNKS = 4
 FUSED = 3
 RUN = 4
 STEEP = 2.0**60
@@ -40,7 +41,7 @@ def as_words(grouped):
     return grouped.rearrange("p (c i) t -> p c t i", i=RUN)
 
 
-VECTOR_BANKS = (0, 0, 1, 0, 0, 2)
+VECTOR_BANKS = (0, 1, 1, 1, 0, 2)
 
 
 def tile_iag_pb_v_kernel(tc, T1, T2, Wf, bn_g, bn_b, z, mu, rstd, grad_out, out):
@@ -87,12 +88,6 @@ def tile_iag_pb_v_kernel(tc, T1, T2, Wf, bn_g, bn_b, z, mu, rstd, grad_out, out)
         ident_bf16 = const.tile([P, P], BF16)
         make_identity(nc, ident_f32[:])
         make_identity(nc, ident_bf16[:])
-        w_grouped = const.tile([P, EMB, PACK], BF16, align_bytes=64)
-        nc.gpsimd.tensor_scalar(
-            out=as_words(w_grouped[:]), in0=by_word(w_planes[:]), scalar1=1.0, scalar2=0.0,
-            op0=ALU.mult, op1=ALU.add,
-        )
-
         cols_f32 = psum.tile([P, P], F32, tag="bank")
         cols_bf16 = psum.tile([P, P], BF16, tag="bank")
         nc.tensor.transpose(out=cols_f32[:], in_=rows_f32[:], identity=ident_f32[:])
@@ -134,6 +129,7 @@ def tile_iag_pb_v_kernel(tc, T1, T2, Wf, bn_g, bn_b, z, mu, rstd, grad_out, out)
 
         gma = [resident.tile([P, PACK, CHUNK], F32, name="gma") for c in range(CHUNKS)]
         sums = const.tile([P, 2, PACK, CHUNKS], F32)
+        nc.vector.memset(sums[:], 0.0)
 
         def transpose_z(c, t):
             bank = psum.tile([P, CHUNK], F32, tag="bank")
@@ -189,6 +185,28 @@ def tile_iag_pb_v_kernel(tc, T1, T2, Wf, bn_g, bn_b, z, mu, rstd, grad_out, out)
                         scale=gain[:, t : t + 1], accum_out=sums[:, 0, t, c : c + 1],
                     )
 
+        row_sums = const.tile([P, PAIR, CHUNK], F32)
+        nc.gpsimd.memset(row_sums[:], 0.0)
+
+        def apply_gain_gpsimd(c, planes, masked):
+            rows = slice(0, P * TILES[c])
+            for k, t in enumerate(planes):
+                nc.gpsimd.tensor_scalar(
+                    out=gma[c][:, t, rows], in0=masked[k], scalar1=gain[:, t : t + 1], scalar2=0.0,
+                    op0=ALU.mult, op1=ALU.add,
+                )
+            nc.gpsimd.tensor_add(
+                out=row_sums[:, :, rows], in0=row_sums[:, :, rows], in1=gma[c][:, 0:PAIR, rows]
+            )
+
+        def add_up_rows():
+            for t in range(PAIR):
+                scaled = stream.tile([P, CHUNK], F32)
+                nc.scalar.activation(
+                    out=scaled[:], in_=row_sums[:, t, :], func=ACT.Identity,
+                    accum_out=sums[:, 0, t, 0:1],
+                )
+
         def correlate(k, c, planes, z_t, masked):
             t = planes[k]
             product = stream.tile([P, CHUNK], F32)
@@ -207,9 +225,14 @@ def tile_iag_pb_v_kernel(tc, T1, T2, Wf, bn_g, bn_b, z, mu, rstd, grad_out, out)
             z_t, g_t = transpose_pair(c, planes)
             mask = make_mask(c, planes, z_t)
             masked = apply_mask(c, planes, mask, g_t)
-            if waiting and i + 1 < len(steps) - 1:
+            if waiting and i + 2 < len(steps):
                 apply_gain(*waiting.pop(0))
-            waiting.append((c, planes, masked))
+            if planes[0] == 0 and c < GPSIMD_CHUNKS:
+                apply_gain_gpsimd(c, planes, masked)
+            else:
+                waiting.append((c, planes, masked))
+            if i + 2 == len(steps):
+                add_up_rows()
             if before is not None:
                 correlate(1, *before)
             if i + 1 == len(steps):
@@ -218,6 +241,12 @@ def tile_iag_pb_v_kernel(tc, T1, T2, Wf, bn_g, bn_b, z, mu, rstd, grad_out, out)
             correlate(0, *before)
         while waiting:
             apply_gain(*waiting.pop(0))
+
+        w_grouped = const.tile([P, EMB, PACK], BF16, align_bytes=64)
+        nc.gpsimd.tensor_scalar(
+            out=as_words(w_grouped[:]), in0=by_word(w_planes[:]), scalar1=1.0, scalar2=0.0,
+            op0=ALU.mult, op1=ALU.add,
+        )
 
         slope = const.tile([P, PACK], F32)
         shift = const.tile([P, PACK], F32)

@@ -131,8 +131,15 @@ def tile_iag_pb_v_kernel(tc, T1, T2, Wf, bn_g, bn_b, z, mu, rstd, grad_out, out)
         sums = const.tile([P, 2, PACK, CHUNKS], F32)
         nc.vector.memset(sums[:], 0.0)
 
-        def transpose_z(c, t):
+        def keep_clock(bank, count):
+            for k in range(count):
+                nc.tensor.matmul(
+                    out=bank[:, 0:P], lhsT=ident_f32[:], rhs=ident_f32[:], start=True, stop=True
+                )
+
+        def transpose_z(c, t, clock_matmuls=0):
             bank = psum.tile([P, CHUNK], F32, tag="bank")
+            keep_clock(bank, clock_matmuls)
             for j in range(TILES[c]):
                 nc.tensor.transpose(
                     out=bank[:, j * P : (j + 1) * P],
@@ -140,8 +147,8 @@ def tile_iag_pb_v_kernel(tc, T1, T2, Wf, bn_g, bn_b, z, mu, rstd, grad_out, out)
                 )
             return bank[:, 0 : P * TILES[c]]
 
-        def transpose_pair(c, planes):
-            z_t = [transpose_z(c, t) for t in planes]
+        def transpose_pair(c, planes, clock_matmuls):
+            z_t = [transpose_z(c, planes[0], clock_matmuls), transpose_z(c, planes[1])]
             g_t = psum.tile([P, PAIR, CHUNK], BF16, tag="bank")
             for k in range(PAIR):
                 for j in range(TILES[c]):
@@ -222,7 +229,7 @@ def tile_iag_pb_v_kernel(tc, T1, T2, Wf, bn_g, bn_b, z, mu, rstd, grad_out, out)
         waiting = []
         before = None
         for i, (c, planes) in enumerate(steps):
-            z_t, g_t = transpose_pair(c, planes)
+            z_t, g_t = transpose_pair(c, planes, (0, 2, 2, 2)[i] if i < 4 else 1)
             mask = make_mask(c, planes, z_t)
             masked = apply_mask(c, planes, mask, g_t)
             if waiting and i + 2 < len(steps):

@@ -229,7 +229,8 @@ def tile_iag_pb_v_kernel(tc, T1, T2, Wf, bn_g, bn_b, z, mu, rstd, grad_out, out)
         waiting = []
         before = None
         for i, (c, planes) in enumerate(steps):
-            z_t, g_t = transpose_pair(c, planes, (0, 2, 2, 2)[i] if i < 4 else 1)
+            clock_matmuls = 0 if c == 0 else 1 if planes[0] else 3 if c == 1 else 2
+            z_t, g_t = transpose_pair(c, planes, clock_matmuls)
             mask = make_mask(c, planes, z_t)
             masked = apply_mask(c, planes, mask, g_t)
             if waiting and i + 2 < len(steps):
@@ -251,7 +252,7 @@ def tile_iag_pb_v_kernel(tc, T1, T2, Wf, bn_g, bn_b, z, mu, rstd, grad_out, out)
 
         w_grouped = const.tile([P, EMB, PACK], BF16, align_bytes=64)
         nc.gpsimd.tensor_scalar(
-            out=as_words(w_grouped[:]), in0=by_word(w_planes[:]), scalar1=1.0, scalar2=0.0,
+            out=w_grouped[:], in0=w_planes[:].rearrange("p t c -> p c t"), scalar1=1.0, scalar2=0.0,
             op0=ALU.mult, op1=ALU.add,
         )
 
@@ -304,7 +305,7 @@ def tile_iag_pb_v_kernel(tc, T1, T2, Wf, bn_g, bn_b, z, mu, rstd, grad_out, out)
         terms = [means.tile([P, PACK, CHUNK], F32, name="terms") for c in range(AHEAD)]
 
         def means_term(c, t):
-            bank = transpose_z(c, t)
+            bank = transpose_z(c, t, 2 if c < AHEAD and t == 0 else 0)
             term = terms[c][:, t, 0 : P * TILES[c]]
             if c == 0 and t >= PAIR:
                 nc.vector.tensor_scalar(

from contextlib import ExitStack

import concourse.mybir as mybir
from concourse.masks import make_identity

F32 = mybir.dt.float32
BF16 = mybir.dt.bfloat16
U32 = mybir.dt.uint32
U8 = mybir.dt.uint8
E5M2_X4 = mybir.dt.float8_e5m2_x4
E4M3_X4 = mybir.dt.float8_e4m3fn_x4
ALU = mybir.AluOpType
ACT = mybir.ActivationFunctionType
AXIS = mybir.AxisListType

P = 128
PACK = 4
EMB = 512
ROWS = 4 * 640
TILES = (2, 3, 4, 4, 4, 3)
CHUNKS = len(TILES)
STARTS = [P * sum(TILES[:c]) for c in range(CHUNKS)]
CHUNK = P * max(TILES)
PAIR = 2
GPSIMD_CHUNKS = 4
FUSED = 3
RUN = 4
STEEP = 2.0**60
FLOOR = 200.0
AHEAD = 2

FLOPS = 2 * ROWS * EMB * EMB
BYTES = ROWS * EMB * (4 + 2 + 4) + EMB * EMB * 2 + EMB * (4 + 4 + 2 + 2)


def by_word(planes):
    return planes.rearrange("p t (c i) -> p c t i", i=RUN)


def as_words(grouped):
    return grouped.rearrange("p (c i) t -> p c t i", i=RUN)


VECTOR_BANKS = (0, 1, 1, 1, 0, 2)


def tile_iag_pb_v_kernel(tc, T1, T2, Wf, bn_g, bn_b, z, mu, rstd, grad_out, out):
    nc = tc.nc

    def in_chunk(rows, c, pattern):
        part = rows.flatten_outer_dims()[STARTS[c] : STARTS[c] + P * TILES[c], :]
        return part.rearrange(pattern, p=P, j=TILES[c])

    with ExitStack() as ctx:
        ctx.enter_context(tc.manual_schedule())
        const = ctx.enter_context(tc.tile_pool(name="const", bufs=1))
        resident = ctx.enter_context(tc.tile_pool(name="resident", bufs=CHUNKS))
        stream = ctx.enter_context(tc.tile_pool(name="stream", bufs=4))
        stage = ctx.enter_context(tc.tile_pool(name="stage", bufs=2))
        means = ctx.enter_context(tc.tile_pool(name="means", bufs=AHEAD + 1))
        outgoing = ctx.enter_context(tc.tile_pool(name="outgoing", bufs=3 * max(TILES)))
        psum = ctx.enter_context(tc.psum_pool(name="psum", bufs=8))

        rows_f32 = const.tile([P, P], F32)
        rows_bf16 = const.tile([P, P], BF16)
        nc.gpsimd.memset(rows_f32[:], 0.0)
        nc.gpsimd.memset(rows_bf16[:], 0.0)
        nc.sync.dma_start(out=rows_f32[0:PACK, :], in_=mu.rearrange("(t p) -> t p", p=P))
        nc.sync.dma_start(out=rows_f32[PACK : 2 * PACK, :], in_=rstd.rearrange("(t p) -> t p", p=P))
        nc.sync.dma_start(out=rows_bf16[0:PACK, :], in_=bn_g.rearrange("(t p) -> t p", p=P))
        nc.sync.dma_start(out=rows_bf16[PACK : 2 * PACK, :], in_=bn_b.rearrange("(t p) -> t p", p=P))

        warm = const.tile([P, 1], F32)
        nc.gpsimd.memset(warm[:], 0.0)
        nc.scalar.activation(out=warm[:], in_=warm[:], func=ACT.Sigmoid)

        z_in = []
        g_in = []
        for c in range(CHUNKS):
            z_in.append(resident.tile([P, max(TILES), EMB], F32, name="z_in"))
            g_in.append(resident.tile([P, max(TILES), EMB], BF16, name="g_in"))
            nc.sync.dma_start(out=z_in[c][:, 0 : TILES[c], :], in_=in_chunk(z, c, "(p j) o -> p j o"))
            nc.sync.dma_start(out=g_in[c][:, 0 : TILES[c], :], in_=in_chunk(grad_out, c, "(p j) o -> p j o"))
        w_planes = const.tile([P, PACK, EMB], BF16)
        nc.sync.dma_start(out=w_planes[:], in_=Wf.rearrange("(t p) c -> p t c", p=P)[:, :, 0:EMB])

        ident_f32 = const.tile([P, P], F32)
        ident_bf16 = const.tile([P, P], BF16)
        make_identity(nc, ident_f32[:])
        make_identity(nc, ident_bf16[:])
        cols_f32 = psum.tile([P, P], F32, tag="bank")
        cols_bf16 = psum.tile([P, P], BF16, tag="bank")
        nc.tensor.transpose(out=cols_f32[:], in_=rows_f32[:], identity=ident_f32[:])
        nc.tensor.transpose(out=cols_bf16[:], in_=rows_bf16[:], identity=ident_bf16[:])
        gain = const.tile([P, PACK], F32)
        stats = const.tile([P, 2 * PACK], F32)
        mean = stats[:, 0:PACK]
        inv_std = stats[:, PACK : 2 * PACK]
        gamma = const.tile([P, PACK], F32)
        steep_beta = const.tile([P, PACK], F32)
        neg_mean = const.tile([P, PACK], F32)
        mask_scale = const.tile([P, PACK], F32)
        mask_bias = const.tile([P, PACK], F32)
        slope_factor = const.tile([P, PACK], F32)
        shift_factor = const.tile([P, PACK], F32)

        nc.vector.tensor_copy(out=gamma[:], in_=cols_bf16[:, 0:PACK])
        nc.vector.tensor_scalar(
            out=steep_beta[:], in0=cols_bf16[:, PACK : 2 * PACK], scalar1=STEEP, scalar2=-FLOOR,
            op0=ALU.mult, op1=ALU.add,
        )
        nc.vector.scalar_tensor_tensor(
            out=mask_scale[:], in0=cols_f32[:, PACK : 2 * PACK], scalar=STEEP, in1=gamma[:],
            op0=ALU.mult, op1=ALU.mult,
        )
        nc.vector.tensor_copy(out=stats[:], in_=cols_f32[:, 0 : 2 * PACK])
        nc.vector.scalar_tensor_tensor(
            out=mask_bias[:], in0=cols_f32[:, 0:PACK], scalar=-1.0, in1=mask_scale[:],
            op0=ALU.mult, op1=ALU.mult,
        )
        nc.vector.tensor_mul(out=gain[:], in0=inv_std, in1=gamma[:])
        nc.vector.tensor_add(out=mask_bias[:], in0=mask_bias[:], in1=steep_beta[:])
        nc.vector.tensor_scalar_mul(out=neg_mean[:], in0=mean, scalar1=-1.0)
        nc.vector.scalar_tensor_tensor(
            out=slope_factor[:], in0=inv_std, scalar=-1.0 / ROWS, in1=inv_std, op0=ALU.mult, op1=ALU.mult
        )
        nc.vector.tensor_mul(out=slope_factor[:, 0:FUSED], in0=slope_factor[:, 0:FUSED], in1=gain[:, 0:FUSED])
        nc.vector.tensor_mul(out=shift_factor[:], in0=slope_factor[:], in1=neg_mean[:])

        gma = [resident.tile([P, PACK, CHUNK], F32, name="gma") for c in range(CHUNKS)]
        sums = const.tile([P, 2, PACK, CHUNKS], F32)
        nc.vector.memset(sums[:], 0.0)

        def keep_clock(bank, count):
            for k in range(count):
                nc.tensor.matmul(
                    out=bank[:, 0:P], lhsT=ident_f32[:], rhs=ident_f32[:], start=True, stop=True
                )

        def transpose_z(c, t, clock_matmuls=0):
            bank = psum.tile([P, CHUNK], F32, tag="bank")
            keep_clock(bank, clock_matmuls)
            for j in range(TILES[c]):
                nc.tensor.transpose(
                    out=bank[:, j * P : (j + 1) * P],
                    in_=z_in[c][:, j, t * P : (t + 1) * P], identity=ident_f32[:],
                )
            return bank[:, 0 : P * TILES[c]]

        def transpose_pair(c, planes, clock_matmuls):
            z_t = [transpose_z(c, planes[0], clock_matmuls), transpose_z(c, planes[1])]
            g_t = psum.tile([P, PAIR, CHUNK], BF16, tag="bank")
            for k in range(PAIR):
                for j in range(TILES[c]):
                    nc.tensor.transpose(
                        out=g_t[:, k, j * P : (j + 1) * P],
                        in_=g_in[c][:, j, planes[k] * P : (planes[k] + 1) * P], identity=ident_bf16[:],
                    )
            return z_t, g_t[:, :, 0 : P * TILES[c]]

        def make_mask(c, planes, z_t):
            mask = stream.tile([P, PAIR, CHUNK], BF16)
            mask = mask[:, :, 0 : P * TILES[c]]
            for k in range(PAIR):
                t = planes[k]
                nc.scalar.activation(
                    out=mask[:, k, :], in_=z_t[k], func=ACT.Sigmoid,
                    scale=mask_scale[:, t : t + 1], bias=mask_bias[:, t : t + 1],
                )
            return mask

        def apply_mask(c, planes, mask, g_t):
            rows = slice(0, P * TILES[c])
            gm = stream.tile([P, PAIR, CHUNK], BF16)
            plain = PAIR - 1 if FUSED in planes else PAIR
            nc.vector.tensor_tensor(
                out=gm[:, 0:plain, rows], in0=mask[:, 0:plain, :], in1=g_t[:, 0:plain, :], op=ALU.mult
            )
            if FUSED in planes:
                nc.vector.scalar_tensor_tensor(
                    out=gma[c][:, FUSED, rows], in0=mask[:, plain, :], scalar=gain[:, FUSED : FUSED + 1],
                    in1=g_t[:, plain, :], op0=ALU.mult, op1=ALU.mult,
                    accum_out=sums[:, 0, FUSED, c : c + 1],
                )
            return [gma[c][:, t, rows] if t == FUSED else gm[:, k, rows] for k, t in enumerate(planes)]

        def apply_gain(c, planes, masked):
            for k, t in enumerate(planes):
                if t != FUSED:
                    nc.scalar.activation(
                        out=gma[c][:, t, 0 : P * TILES[c]], in_=masked[k], func=ACT.Identity,
                        scale=gain[:, t : t + 1], accum_out=sums[:, 0, t, c : c + 1],
                    )

        row_sums = const.tile([P, PAIR, CHUNK], F32)
        nc.gpsimd.memset(row_sums[:], 0.0)

        def apply_gain_gpsimd(c, planes, masked):
            rows = slice(0, P * TILES[c])
            for k, t in enumerate(planes):
                nc.gpsimd.tensor_scalar(
                    out=gma[c][:, t, rows], in0=masked[k], scalar1=gain[:, t : t + 1], scalar2=0.0,
                    op0=ALU.mult, op1=ALU.add,
                )
            nc.gpsimd.tensor_add(
                out=row_sums[:, :, rows], in0=row_sums[:, :, rows], in1=gma[c][:, 0:PAIR, rows]
            )

        def add_up_rows():
            for t in range(PAIR):
                scaled = stream.tile([P, CHUNK], F32)
                nc.scalar.activation(
                    out=scaled[:], in_=row_sums[:, t, :], func=ACT.Identity,
                    accum_out=sums[:, 0, t, 0:1],
                )

        def correlate(k, c, planes, z_t, masked):
            t = planes[k]
            product = stream.tile([P, CHUNK], F32)
            nc.vector.scalar_tensor_tensor(
                out=product[:, 0 : P * TILES[c]], in0=z_t[k], scalar=mean[:, t : t + 1], in1=masked[k],
                op0=ALU.subtract, op1=ALU.mult, accum_out=sums[:, 1, t, c : c + 1],
            )

        pairs = ((0, 1), (2, 3))
        steps = [(c, planes) for c in range(CHUNKS) for planes in pairs]
        late = slice(PAIR, PACK)
        known = const.tile([P, PAIR], F32)
        waiting = []
        before = None
        for i, (c, planes) in enumerate(steps):
            clock_matmuls = 0 if c == 0 else 1 if planes[0] else 3 if c == 1 else 2
            z_t, g_t = transpose_pair(c, planes, clock_matmuls)
            mask = make_mask(c, planes, z_t)
            masked = apply_mask(c, planes, mask, g_t)
            if waiting and i + 2 < len(steps):
                apply_gain(*waiting.pop(0))
            if planes[0] == 0 and c < GPSIMD_CHUNKS:
                apply_gain_gpsimd(c, planes, masked)
            else:
                waiting.append((c, planes, masked))
            if i + 2 == len(steps):
                add_up_rows()
            if before is not None:
                correlate(1, *before)
            if i + 1 == len(steps):
                nc.vector.reduce_sum(out=known[:], in_=sums[:, 1, late, 0 : CHUNKS - 1], axis=AXIS.X)
            before = (c, planes, z_t, masked)
            correlate(0, *before)
        while waiting:
            apply_gain(*waiting.pop(0))

        w_grouped = const.tile([P, EMB, PACK], BF16, align_bytes=64)
        nc.gpsimd.tensor_scalar(
            out=w_grouped[:], in0=w_planes[:].rearrange("p t c -> p c t"), scalar1=1.0, scalar2=0.0,
            op0=ALU.mult, op1=ALU.add,
        )

        slope = const.tile([P, PACK], F32)
        shift = const.tile([P, PACK], F32)
        minus_mean = const.tile([P, PAIR], F32)
        total = const.tile([P, PAIR], F32)
        part = const.tile([P, PAIR], F32)
        base = const.tile([P, PAIR], F32)
        nc.vector.tensor_mul(out=part[:], in0=known[:], in1=shift_factor[:, late])
        nc.vector.reduce_sum(out=total[:], in_=sums[:, 0, late, :], axis=AXIS.X)
        nc.vector.scalar_tensor_tensor(
            out=base[:], in0=total[:], scalar=-1.0 / ROWS, in1=part[:], op0=ALU.mult, op1=ALU.add
        )

        def finish(t):
            last = sums[:, 1, t, CHUNKS - 1 : CHUNKS]
            k = t - PAIR
            nc.vector.scalar_tensor_tensor(
                out=slope[:, t : t + 1], in0=last, scalar=known[:, k : k + 1],
                in1=slope_factor[:, t : t + 1], op0=ALU.add, op1=ALU.mult,
            )
            nc.vector.scalar_tensor_tensor(
                out=shift[:, t : t + 1], in0=last, scalar=shift_factor[:, t : t + 1],
                in1=base[:, k : k + 1], op0=ALU.mult, op1=ALU.add,
            )

        finish(2)
        correlate(1, *before)
        for t in pairs[0]:
            scaled = stream.tile([P, CHUNKS], F32)
            nc.scalar.activation(
                out=scaled[:], in_=sums[:, 0, t, :], func=ACT.Identity,
                scale=-1.0 / ROWS, accum_out=minus_mean[:, t : t + 1],
            )
        for t in pairs[0]:
            scaled = stream.tile([P, CHUNKS], F32)
            nc.scalar.activation(
                out=scaled[:], in_=sums[:, 1, t, :], func=ACT.Identity,
                scale=slope_factor[:, t : t + 1], accum_out=slope[:, t : t + 1],
            )
        for t in pairs[0]:
            nc.scalar.activation(
                out=shift[:, t : t + 1], in_=slope[:, t : t + 1], func=ACT.Identity,
                scale=neg_mean[:, t : t + 1], bias=minus_mean[:, t : t + 1],
            )
        w_codes = const.tile([P, EMB], U32, align_bytes=64)
        w_scales = const.tile([P, EMB], U8, align_bytes=64)

        terms = [means.tile([P, PACK, CHUNK], F32, name="terms") for c in range(AHEAD)]

        def means_term(c, t):
            bank = transpose_z(c, t, 2 if c < AHEAD and t == 0 else 0)
            term = terms[c][:, t, 0 : P * TILES[c]]
            if c == 0 and t >= PAIR:
                nc.vector.tensor_scalar(
                    out=term, in0=bank, scalar1=slope[:, t : t + 1], scalar2=shift[:, t : t + 1],
                    op0=ALU.mult, op1=ALU.add,
                )
            else:
                nc.scalar.activation(
                    out=term, in_=bank, func=ACT.Identity,
                    scale=slope[:, t : t + 1], bias=shift[:, t : t + 1],
                )

        def empty(c, j, acc, copy):
            result = outgoing.tile([P, EMB], F32)
            copy(out=result[:], in_=acc[:])
            nc.sync.dma_start(out=in_chunk(out, c, "(p j) o -> j p o")[j], in_=result[:])

        for t in range(PACK):
            if t == 3:
                finish(t)
            means_term(0, t)
        for t in range(PACK):
            means_term(1, t)
        for_vector = []
        for c in range(CHUNKS):
            pieces = ((0, 2 * P), (2 * P, 3 * P)) if TILES[c] == 3 else ((0, P * TILES[c]),)
            spans = [slice(a, b) for a, b in (pieces if c == CHUNKS - 1 else ((0, P * TILES[c]),))]
            dz_grouped = stage.tile([P, CHUNK, PACK], BF16, align_bytes=64)
            for rows in spans:
                nc.vector.tensor_tensor(
                    out=as_words(dz_grouped[:, rows, :]), in0=by_word(gma[c][:, :, rows]),
                    in1=by_word(terms[c][:, :, rows]), op=ALU.add,
                )
            if c + AHEAD < CHUNKS:
                terms.append(means.tile([P, PACK, CHUNK], F32, name="terms"))
                for t in range(PACK):
                    means_term(c + AHEAD, t)
            if c == 0:
                nc.vector.quantize_mx(
                    out=w_codes[:].bitcast(E4M3_X4), scales=w_scales[:],
                    in_=w_grouped[:].rearrange("p c t -> p (c t)"),
                )
            for j, acc in for_vector:
                empty(c - 1, j, acc, nc.vector.tensor_copy)
            dz_codes = stage.tile([P, CHUNK], U32, align_bytes=64)
            dz_scales = stage.tile([P, CHUNK], U8, align_bytes=64)
            for a, b in pieces:
                rows = slice(a, b)
                nc.vector.quantize_mx(
                    out=dz_codes[:, rows].bitcast(E5M2_X4), scales=dz_scales[:, rows],
                    in_=dz_grouped[:, rows, :].rearrange("p w t -> p (w t)"),
                )
            for_vector = []
            for j in range(TILES[c]):
                rows = slice(j * P, (j + 1) * P)
                acc = psum.tile([P, EMB], F32, tag="bank")
                nc.tensor.matmul_mx(
                    out=acc[:],
                    lhsT=dz_codes[:, rows].bitcast(E5M2_X4), lhsT_scale=dz_scales[:, rows],
                    rhs=w_codes[:].bitcast(E4M3_X4), rhs_scale=w_scales[:],
                    start=True, stop=True,
                )
                if j < TILES[c] - VECTOR_BANKS[c]:
                    empty(c, j, acc, nc.scalar.copy)
                else:
                    for_vector.append((j, acc))
        for j, acc in for_vector:
            empty(CHUNKS - 1, j, acc, nc.vector.tensor_copy)
